import numpy as np
import ml_dtypes


def mxq(x, axis, fmt="e4m3"):
    dtype, down = {"e4m3": (ml_dtypes.float8_e4m3fn, 7), "e5m2": (ml_dtypes.float8_e5m2, 14)}[fmt]
    v = np.moveaxis(np.asarray(x, np.float32).astype(ml_dtypes.bfloat16).astype(np.float64), axis, -1)
    blocks = v.reshape(v.shape[:-1] + (-1, 32))
    amax = np.abs(blocks).max(-1, keepdims=True)
    byte = np.maximum(np.where(amax > 0, np.frexp(amax)[1] - 1 + 127, 0) - down, 1)
    scale = np.exp2(byte - 127.0)
    codes = (blocks / scale).astype(np.float32).astype(dtype).astype(np.float64)
    return np.moveaxis((codes * scale).reshape(v.shape), -1, axis)


BF16 = ml_dtypes.bfloat16


def bf(x):
    return np.asarray(x, np.float32).astype(BF16)


def f64(x):
    return np.asarray(x).astype(np.float64)


B, P, C, H = 2, 2048, 512, 8
WD = P // H
GS = 2.0


def setup_inputs():
    return {"qkv_bn": bf(np.random.standard_normal((B, C, P)) * GS / np.sqrt(np.sqrt(WD))),
            "gra_sharp": bf(GS * (1.0 + 0.1 * np.random.standard_normal(1)))}


def reference(qkv_bn, gra_sharp):
    q = f64(qkv_bn).reshape(B, C, H, WD).transpose(0, 2, 1, 3)
    scores = q @ q.transpose(0, 1, 3, 2) / f64(gra_sharp)
    e = np.exp(scores - scores.max(1, keepdims=True))
    attn = e / e.sum(1, keepdims=True)
    o = mxq(attn, 3, "e4m3") @ mxq(q, 2, "e4m3")
    h = o.transpose(0, 2, 1, 3).reshape(B, C, P).transpose(0, 2, 1)
    return h, attn

@@ -1,0 +1,314 @@
+from contextlib import ExitStack
+
+import concourse.mybir as mybir
+from concourse.masks import make_identity
+
+F32 = mybir.dt.float32
+BF16 = mybir.dt.bfloat16
+U32 = mybir.dt.uint32
+U8 = mybir.dt.uint8
+FP8X4 = mybir.dt.float8_e4m3fn_x4
+ALU = mybir.AluOpType
+ACT = mybir.ActivationFunctionType
+AXIS = mybir.AxisListType
+
+P = 128
+BATCH, CHANNELS, TOKENS, HEADS = 2, 512, 2048, 8
+HEAD_TOKENS = TOKENS // HEADS
+CT = CHANNELS // P
+KT = HEAD_TOKENS // P
+TOKEN_TILES = TOKENS // P
+BANK_HEADS = 4
+BANKS = HEADS // BANK_HEADS
+PANEL_TILES = 2
+PANELS = CT // PANEL_TILES
+PAIR = 2
+Q_PIECES = 4
+Q_PIECE_TOKENS = TOKENS // Q_PIECES
+
+UNITS = [(b, i, j) for b in range(BATCH) for i in range(CT) for j in range(i, CT)]
+BATCH_UNITS = len(UNITS) // BATCH
+
+AHEAD_SCORES = 1
+LAG_EXP = 1
+LAG_SUM = 2
+LAG_RECIPROCAL = 3
+LAG_NORMALISE = 4
+LAG_MIRROR = 5
+LOAD_AT = -6
+TURN_AT = -2
+PIECES_PER_STEP = 2
+FIRST_STEP = LOAD_AT
+LAST_STEP = len(UNITS) + LAG_MIRROR + HEADS // PAIR // PIECES_PER_STEP + 4
+
+FLOPS = 2 * 2 * BATCH * HEADS * CHANNELS * CHANNELS * HEAD_TOKENS
+
+
+def tile_channelgroupattention_pa_t_kernel(tc, qkv_bn, gra_sharp, out_0, out_1):
+    nc = tc.nc
+    with ExitStack() as stack:
+        const = stack.enter_context(tc.tile_pool(name="const", bufs=1))
+        natural = stack.enter_context(tc.tile_pool(name="natural", bufs=1))
+        turned = stack.enter_context(tc.tile_pool(name="turned", bufs=2))
+        q_mx = stack.enter_context(tc.tile_pool(name="q_mx", bufs=2))
+        stage = stack.enter_context(tc.tile_pool(name="stage", bufs=2))
+        panels = stack.enter_context(tc.tile_pool(name="panels", bufs=3))
+        work = stack.enter_context(tc.tile_pool(name="work", bufs=2))
+        a_mx = stack.enter_context(tc.tile_pool(name="a_mx", bufs=5))
+        h_pool = stack.enter_context(tc.tile_pool(name="h_pool", bufs=4))
+        psum = stack.enter_context(tc.psum_pool(name="psum", bufs=2))
+        stack.enter_context(tc.manual_schedule())
+
+        ident_bf = const.tile([P, P], BF16)
+        make_identity(nc, ident_bf[:])
+        ident_f32 = const.tile([P, P], F32)
+        make_identity(nc, ident_f32[:])
+
+        sharp_bf = const.tile([P, 1], BF16)
+        nc.sync.dma_start(out=sharp_bf[:], in_=gra_sharp.partition_broadcast(P))
+        sharp = const.tile([P, 1], F32)
+        nc.vector.tensor_copy(out=sharp[:], in_=sharp_bf[:])
+        inv_sharp = const.tile([P, 1], F32)
+        nc.vector.reciprocal(out=inv_sharp[:], in_=sharp[:])
+
+        warm = const.tile([P, 1], F32)
+        nc.vector.memset(warm[:], 0.0)
+        nc.scalar.activation(out=warm[:], in_=warm[:], func=ACT.Exp)
+
+        q_nat, q_t, q_codes, q_scales, panel = {}, {}, {}, {}, {}
+        banks, e, total, share = {}, {}, {}, {}
+        row_fill, column_fill = {}, {}
+
+        def load_q(b):
+            q_nat[b] = natural.tile([P, CT, TOKENS], BF16, name="q_nat")
+            for t in range(CT):
+                nc.sync.dma_start(out=q_nat[b][:, t, :], in_=qkv_bn[b, t * P : (t + 1) * P, :])
+            q_t[b] = turned.tile([P, TOKEN_TILES, CHANNELS], BF16, name="q_t")
+            q_codes[b] = q_mx.tile([P, TOKENS], U32, name="q_codes", align_bytes=64)
+            q_scales[b] = q_mx.tile([P, TOKENS], U8, name="q_scales", align_bytes=64)
+
+        def turn_q(b, t):
+            for g in range(TOKEN_TILES // 4):
+                flipped = psum.tile([P, 4, P], BF16, tag="flip")
+                for k in range(4):
+                    m = 4 * g + k
+                    nc.tensor.transpose(
+                        flipped[:, k, :], q_nat[b][:, t, m * P : (m + 1) * P], ident_bf[:]
+                    )
+                target = q_t[b][:, 4 * g : 4 * g + 4, t * P : (t + 1) * P]
+                if g % 2 == 0:
+                    nc.scalar.copy(out=target, in_=flipped[:])
+                else:
+                    nc.vector.tensor_copy(out=target, in_=flipped[:])
+
+        def quantise_q(b, piece):
+            cols = slice(piece * Q_PIECE_TOKENS, (piece + 1) * Q_PIECE_TOKENS)
+            q_grouped = stage.tile([P, Q_PIECE_TOKENS, CT], BF16, align_bytes=64)
+            nc.vector.tensor_copy(
+                out=q_grouped[:], in_=q_nat[b][:, :, cols].rearrange("p t w -> p w t")
+            )
+            nc.vector.quantize_mx(
+                out=q_codes[b][:, cols].bitcast(FP8X4),
+                scales=q_scales[b][:, cols],
+                in_=q_grouped[:].rearrange("p w t -> p (w t)"),
+            )
+
+        def block_of(b, t, j):
+            first = (j % PANEL_TILES) * P
+            return panel[b][j // PANEL_TILES][:, t, :, first : first + P]
+
+        def scores(u):
+            b, i, j = UNITS[u]
+            banks[u] = []
+            for half in range(BANKS):
+                bank = psum.tile([P, BANK_HEADS, P], F32, tag="scores", bufs=4)
+                for k in range(BANK_HEADS):
+                    for kt in range(KT):
+                        m = (half * BANK_HEADS + k) * KT + kt
+                        nc.tensor.matmul(
+                            bank[:, k, :],
+                            lhsT=q_t[b][:, m, i * P : (i + 1) * P],
+                            rhs=q_t[b][:, m, j * P : (j + 1) * P],
+                            start=(kt == 0),
+                            stop=(kt == KT - 1),
+                        )
+                banks[u].append(bank)
+
+        def subtract_maximum(u):
+            bank_top = work.tile([P, BANKS, P], F32)
+            for half in range(BANKS):
+                nc.vector.tensor_reduce(
+                    out=bank_top[:, half, :],
+                    in_=banks[u][half][:].rearrange("p n d -> p d n"),
+                    axis=AXIS.X,
+                    op=ALU.max,
+                )
+            top = work.tile([P, P], F32)
+            nc.vector.tensor_tensor(
+                out=top[:], in0=bank_top[:, 0, :], in1=bank_top[:, 1, :], op=ALU.max
+            )
+            e[u] = work.tile([P, HEADS, P], F32, name="e", bufs=LAG_NORMALISE + 1)
+            for half in range(BANKS):
+                nc.vector.tensor_tensor(
+                    out=e[u][:, half * BANK_HEADS : (half + 1) * BANK_HEADS, :],
+                    in0=banks[u][half][:],
+                    in1=top[:].unsqueeze(1).to_broadcast([P, BANK_HEADS, P]),
+                    op=ALU.subtract,
+                )
+
+        def exponential(u):
+            nc.scalar.activation(out=e[u][:], in_=e[u][:], func=ACT.Exp, scale=inv_sharp[:, 0:1])
+
+        def sum_heads(u):
+            sum4 = work.tile([P, 4, P], F32)
+            nc.gpsimd.tensor_tensor(
+                out=sum4[:], in0=e[u][:, 0:4, :], in1=e[u][:, 4:8, :], op=ALU.add
+            )
+            sum2 = work.tile([P, 2, P], F32)
+            nc.gpsimd.tensor_tensor(
+                out=sum2[:], in0=sum4[:, 0:2, :], in1=sum4[:, 2:4, :], op=ALU.add
+            )
+            total[u] = work.tile([P, P], F32, name="total", bufs=3)
+            nc.gpsimd.tensor_tensor(
+                out=total[u][:], in0=sum2[:, 0, :], in1=sum2[:, 1, :], op=ALU.add
+            )
+
+        def reciprocal(u):
+            share[u] = work.tile([P, P], F32, name="share", bufs=3)
+            nc.vector.reciprocal(out=share[u][:], in_=total[u][:])
+
+        def normalise(u):
+            b, i, j = UNITS[u]
+            if u % BATCH_UNITS == 0:
+                panel[b] = [
+                    panels.tile([P, CT, HEADS, PANEL_TILES * P], F32, name="panel", tag="panel")
+                    for J in range(PANELS)
+                ]
+                row_fill[b] = [[0] * CT for J in range(PANELS)]
+                column_fill[b] = [0] * CT
+            nc.gpsimd.tensor_tensor(
+                out=block_of(b, i, j),
+                in0=e[u][:],
+                in1=share[u][:].unsqueeze(1).to_broadcast([P, HEADS, P]),
+                op=ALU.mult,
+            )
+
+        def mirror(u):
+            b, i, j = UNITS[u]
+            for half in range(BANKS):
+                heads = slice(half * BANK_HEADS, (half + 1) * BANK_HEADS)
+                flipped = psum.tile([P, BANK_HEADS, P], F32, tag="flip")
+                for k in range(BANK_HEADS):
+                    nc.tensor.transpose(
+                        flipped[:, k, :],
+                        block_of(b, i, j)[:, half * BANK_HEADS + k, :],
+                        ident_f32[:],
+                    )
+                nc.scalar.copy(out=block_of(b, j, i)[:, heads, :], in_=flipped[:])
+
+        def block_written(b, t, j):
+            J = j // PANEL_TILES
+            width = PANEL_TILES * P
+            row_fill[b][J][t] += 1
+            if row_fill[b][J][t] == PANEL_TILES:
+                attn_rows = out_1[b].rearrange("n (t p) d -> p t n d", p=P)
+                nc.sync.dma_start(
+                    out=attn_rows[:, t, :, J * width : (J + 1) * width], in_=panel[b][J][:, t, :, :]
+                )
+            column_fill[b][j] += 1
+            if column_fill[b][j] == CT:
+                return [(b, j, pair) for pair in range(HEADS // PAIR)]
+            return []
+
+        def regroup(piece):
+            b, j, pair = piece
+            first = (j % PANEL_TILES) * P
+            heads = slice(pair * PAIR, (pair + 1) * PAIR)
+            by_word = panel[b][j // PANEL_TILES][:, :, heads, first : first + P].rearrange(
+                "p t n c -> p n c t"
+            )
+            a_grouped = a_mx.tile([P, PAIR, P, CT], BF16, align_bytes=64)
+            if pair % 2 == 0:
+                nc.vector.tensor_copy(out=a_grouped[:], in_=by_word)
+            else:
+                nc.scalar.copy(out=a_grouped[:], in_=by_word)
+            return piece, a_grouped
+
+        def quantise(piece, a_grouped):
+            a_codes = a_mx.tile([P, PAIR * P], U32, align_bytes=64)
+            a_scales = a_mx.tile([P, PAIR * P], U8, align_bytes=64)
+            nc.vector.quantize_mx(
+                out=a_codes[:].bitcast(FP8X4),
+                scales=a_scales[:],
+                in_=a_grouped[:].rearrange("p n c t -> p (n c t)"),
+            )
+            return piece, a_codes, a_scales
+
+        def multiply(piece, a_codes, a_scales):
+            b, j, pair = piece
+            acc = psum.tile([P, PAIR * KT, P], F32, tag="acc")
+            for k in range(PAIR * KT):
+                m = pair * PAIR * KT + k
+                n = k // KT
+                nc.tensor.matmul_mx(
+                    out=acc[:, k, :],
+                    lhsT=q_codes[b][:, m * P : (m + 1) * P].bitcast(FP8X4),
+                    lhsT_scale=q_scales[b][:, m * P : (m + 1) * P],
+                    rhs=a_codes[:, n * P : (n + 1) * P].bitcast(FP8X4),
+                    rhs_scale=a_scales[:, n * P : (n + 1) * P],
+                    start=True,
+                    stop=True,
+                )
+            return piece, acc
+
+        def store_h(piece, acc):
+            b, j, pair = piece
+            h_sb = h_pool.tile([P, PAIR * KT, P], F32)
+            nc.scalar.copy(out=h_sb[:], in_=acc[:])
+            h_rows = out_0[b].rearrange("(m w) c -> w m c", w=P)
+            first = pair * PAIR * KT
+            nc.sync.dma_start(
+                out=h_rows[:, first : first + PAIR * KT, j * P : (j + 1) * P], in_=h_sb[:]
+            )
+
+        def is_unit(u):
+            return 0 <= u < len(UNITS)
+
+        waiting, regrouped, quantised, multiplied = [], [], [], []
+        for step in range(FIRST_STEP, LAST_STEP):
+            if is_unit(step - LAG_MIRROR) and UNITS[step - LAG_MIRROR][1] != UNITS[step - LAG_MIRROR][2]:
+                mirror(step - LAG_MIRROR)
+            if is_unit(step + AHEAD_SCORES):
+                scores(step + AHEAD_SCORES)
+            if is_unit(step - LAG_RECIPROCAL):
+                reciprocal(step - LAG_RECIPROCAL)
+            if is_unit(step - LAG_EXP):
+                exponential(step - LAG_EXP)
+            if is_unit(step - LAG_NORMALISE):
+                normalise(step - LAG_NORMALISE)
+            if is_unit(step - LAG_SUM):
+                sum_heads(step - LAG_SUM)
+            for item in multiplied:
+                store_h(*item)
+            if is_unit(step - LAG_MIRROR):
+                b, i, j = UNITS[step - LAG_MIRROR]
+                waiting.extend(block_written(b, i, j))
+                if i != j:
+                    waiting.extend(block_written(b, j, i))
+            multiplied = [multiply(*item) for item in quantised]
+            quantised = [quantise(*item) for item in regrouped]
+            regrouped = [regroup(piece) for piece in waiting[:PIECES_PER_STEP]]
+            waiting = waiting[PIECES_PER_STEP:]
+            for b in range(BATCH):
+                since = step - b * BATCH_UNITS
+                if 0 <= since < Q_PIECES:
+                    quantise_q(b, since)
+            if is_unit(step):
+                subtract_maximum(step)
+            for b in range(BATCH):
+                since = step - b * BATCH_UNITS
+                if 0 <= since - TURN_AT < CT:
+                    turn_q(b, since - TURN_AT)
+                if since == LOAD_AT:
+                    load_q(b)
+        assert not (waiting or regrouped or quantised or multiplied)

@@ -22,7 +22,7 @@ BANK_HEADS = 4
 BANKS = HEADS // BANK_HEADS
 PANEL_TILES = 2
 PANELS = CT // PANEL_TILES
-PAIR = 2
+PIECE_HEADS = 4
 Q_PIECES = 4
 Q_PIECE_TOKENS = TOKENS // Q_PIECES
 
@@ -37,9 +37,9 @@ LAG_NORMALISE = 4
 LAG_MIRROR = 5
 LOAD_AT = -6
 TURN_AT = -2
-PIECES_PER_STEP = 2
+PIECES_PER_STEP = 1
 FIRST_STEP = LOAD_AT
-LAST_STEP = len(UNITS) + LAG_MIRROR + HEADS // PAIR // PIECES_PER_STEP + 4
+LAST_STEP = len(UNITS) + LAG_MIRROR + 2 * HEADS // PIECE_HEADS // PIECES_PER_STEP + 4
 
 FLOPS = 2 * 2 * BATCH * HEADS * CHANNELS * CHANNELS * HEAD_TOKENS
 
@@ -54,8 +54,8 @@ def tile_channelgroupattention_pa_t_kernel(tc, qkv_bn, gra_sharp, out_0, out_1):
         stage = stack.enter_context(tc.tile_pool(name="stage", bufs=2))
         panels = stack.enter_context(tc.tile_pool(name="panels", bufs=3))
         work = stack.enter_context(tc.tile_pool(name="work", bufs=2))
-        a_mx = stack.enter_context(tc.tile_pool(name="a_mx", bufs=5))
-        h_pool = stack.enter_context(tc.tile_pool(name="h_pool", bufs=4))
+        a_mx = stack.enter_context(tc.tile_pool(name="a_mx", bufs=2))
+        h_pool = stack.enter_context(tc.tile_pool(name="h_pool", bufs=2))
         psum = stack.enter_context(tc.psum_pool(name="psum", bufs=2))
         stack.enter_context(tc.manual_schedule())
 
@@ -75,7 +75,7 @@ def tile_channelgroupattention_pa_t_kernel(tc, qkv_bn, gra_sharp, out_0, out_1):
         nc.vector.memset(warm[:], 0.0)
         nc.scalar.activation(out=warm[:], in_=warm[:], func=ACT.Exp)
 
-        q_nat, q_t, q_codes, q_scales, panel = {}, {}, {}, {}, {}
+        q_nat, q_t, q_grouped, q_codes, q_scales, panel = {}, {}, {}, {}, {}, {}
         banks, e, total, share = {}, {}, {}, {}
         row_fill, column_fill = {}, {}
 
@@ -101,16 +101,21 @@ def tile_channelgroupattention_pa_t_kernel(tc, qkv_bn, gra_sharp, out_0, out_1):
                 else:
                     nc.vector.tensor_copy(out=target, in_=flipped[:])
 
+        def regroup_q(b, piece):
+            cols = slice(piece * Q_PIECE_TOKENS, (piece + 1) * Q_PIECE_TOKENS)
+            q_grouped[b, piece] = stage.tile(
+                [P, Q_PIECE_TOKENS, CT], BF16, name="q_grouped", align_bytes=64
+            )
+            nc.scalar.copy(
+                out=q_grouped[b, piece][:], in_=q_nat[b][:, :, cols].rearrange("p t w -> p w t")
+            )
+
         def quantise_q(b, piece):
             cols = slice(piece * Q_PIECE_TOKENS, (piece + 1) * Q_PIECE_TOKENS)
-            q_grouped = stage.tile([P, Q_PIECE_TOKENS, CT], BF16, align_bytes=64)
-            nc.vector.tensor_copy(
-                out=q_grouped[:], in_=q_nat[b][:, :, cols].rearrange("p t w -> p w t")
-            )
             nc.vector.quantize_mx(
                 out=q_codes[b][:, cols].bitcast(FP8X4),
                 scales=q_scales[b][:, cols],
-                in_=q_grouped[:].rearrange("p w t -> p (w t)"),
+                in_=q_grouped[b, piece][:].rearrange("p w t -> p (w t)"),
             )
 
         def block_of(b, t, j):
@@ -144,8 +149,8 @@ def tile_channelgroupattention_pa_t_kernel(tc, qkv_bn, gra_sharp, out_0, out_1):
                     op=ALU.max,
                 )
             top = work.tile([P, P], F32)
-            nc.vector.tensor_tensor(
-                out=top[:], in0=bank_top[:, 0, :], in1=bank_top[:, 1, :], op=ALU.max
+            nc.vector.tensor_reduce(
+                out=top[:], in_=bank_top[:].rearrange("p h d -> p d h"), axis=AXIS.X, op=ALU.max
             )
             e[u] = work.tile([P, HEADS, P], F32, name="e", bufs=LAG_NORMALISE + 1)
             for half in range(BANKS):
@@ -217,26 +222,23 @@ def tile_channelgroupattention_pa_t_kernel(tc, qkv_bn, gra_sharp, out_0, out_1):
                 )
             column_fill[b][j] += 1
             if column_fill[b][j] == CT:
-                return [(b, j, pair) for pair in range(HEADS // PAIR)]
+                return [(b, j, part) for part in range(HEADS // PIECE_HEADS)]
             return []
 
         def regroup(piece):
-            b, j, pair = piece
+            b, j, part = piece
             first = (j % PANEL_TILES) * P
-            heads = slice(pair * PAIR, (pair + 1) * PAIR)
+            heads = slice(part * PIECE_HEADS, (part + 1) * PIECE_HEADS)
             by_word = panel[b][j // PANEL_TILES][:, :, heads, first : first + P].rearrange(
                 "p t n c -> p n c t"
             )
-            a_grouped = a_mx.tile([P, PAIR, P, CT], BF16, align_bytes=64)
-            if pair % 2 == 0:
-                nc.vector.tensor_copy(out=a_grouped[:], in_=by_word)
-            else:
-                nc.scalar.copy(out=a_grouped[:], in_=by_word)
+            a_grouped = a_mx.tile([P, PIECE_HEADS, P, CT], BF16, align_bytes=64)
+            nc.scalar.copy(out=a_grouped[:], in_=by_word)
             return piece, a_grouped
 
         def quantise(piece, a_grouped):
-            a_codes = a_mx.tile([P, PAIR * P], U32, align_bytes=64)
-            a_scales = a_mx.tile([P, PAIR * P], U8, align_bytes=64)
+            a_codes = a_mx.tile([P, PIECE_HEADS * P], U32, align_bytes=64)
+            a_scales = a_mx.tile([P, PIECE_HEADS * P], U8, align_bytes=64)
             nc.vector.quantize_mx(
                 out=a_codes[:].bitcast(FP8X4),
                 scales=a_scales[:],
@@ -245,30 +247,34 @@ def tile_channelgroupattention_pa_t_kernel(tc, qkv_bn, gra_sharp, out_0, out_1):
             return piece, a_codes, a_scales
 
         def multiply(piece, a_codes, a_scales):
-            b, j, pair = piece
-            acc = psum.tile([P, PAIR * KT, P], F32, tag="acc")
-            for k in range(PAIR * KT):
-                m = pair * PAIR * KT + k
-                n = k // KT
-                nc.tensor.matmul_mx(
-                    out=acc[:, k, :],
-                    lhsT=q_codes[b][:, m * P : (m + 1) * P].bitcast(FP8X4),
-                    lhsT_scale=q_scales[b][:, m * P : (m + 1) * P],
-                    rhs=a_codes[:, n * P : (n + 1) * P].bitcast(FP8X4),
-                    rhs_scale=a_scales[:, n * P : (n + 1) * P],
-                    start=True,
-                    stop=True,
-                )
-            return piece, acc
+            b, j, part = piece
+            accs = []
+            for half in range(PIECE_HEADS * KT // 4):
+                acc = psum.tile([P, 4, P], F32, tag="acc")
+                for k in range(4):
+                    n = (half * 4 + k) // KT
+                    m = part * PIECE_HEADS * KT + half * 4 + k
+                    nc.tensor.matmul_mx(
+                        out=acc[:, k, :],
+                        lhsT=q_codes[b][:, m * P : (m + 1) * P].bitcast(FP8X4),
+                        lhsT_scale=q_scales[b][:, m * P : (m + 1) * P],
+                        rhs=a_codes[:, n * P : (n + 1) * P].bitcast(FP8X4),
+                        rhs_scale=a_scales[:, n * P : (n + 1) * P],
+                        start=True,
+                        stop=True,
+                    )
+                accs.append(acc)
+            return piece, accs
 
-        def store_h(piece, acc):
-            b, j, pair = piece
-            h_sb = h_pool.tile([P, PAIR * KT, P], F32)
-            nc.scalar.copy(out=h_sb[:], in_=acc[:])
+        def store_h(piece, accs):
+            b, j, part = piece
+            tiles = PIECE_HEADS * KT
+            h_sb = h_pool.tile([P, tiles, P], F32)
+            for half in range(tiles // 4):
+                nc.vector.tensor_copy(out=h_sb[:, half * 4 : (half + 1) * 4, :], in_=accs[half][:])
             h_rows = out_0[b].rearrange("(m w) c -> w m c", w=P)
-            first = pair * PAIR * KT
             nc.sync.dma_start(
-                out=h_rows[:, first : first + PAIR * KT, j * P : (j + 1) * P], in_=h_sb[:]
+                out=h_rows[:, part * tiles : (part + 1) * tiles, j * P : (j + 1) * P], in_=h_sb[:]
             )
 
         def is_unit(u):
@@ -301,8 +307,10 @@ def tile_channelgroupattention_pa_t_kernel(tc, qkv_bn, gra_sharp, out_0, out_1):
             waiting = waiting[PIECES_PER_STEP:]
             for b in range(BATCH):
                 since = step - b * BATCH_UNITS
+                if 0 <= since - 1 < Q_PIECES:
+                    quantise_q(b, since - 1)
                 if 0 <= since < Q_PIECES:
-                    quantise_q(b, since)
+                    regroup_q(b, since)
             if is_unit(step):
                 subtract_maximum(step)
             for b in range(BATCH):

@@ -20,6 +20,7 @@ KT = HEAD_TOKENS // P
 TOKEN_TILES = TOKENS // P
 BANK_HEADS = 4
 BANKS = HEADS // BANK_HEADS
+BANK_COLUMNS = P // BANKS
 PANEL_TILES = 2
 PANELS = CT // PANEL_TILES
 PIECE_HEADS = 4
@@ -32,13 +33,10 @@ BATCH_UNITS = len(UNITS) // BATCH
 AHEAD_SCORES = 1
 LAG_EXP = 1
 LAG_SUM = 2
-LAG_RECIPROCAL = 3
-LAG_NORMALISE = 4
-LAG_MIRROR = 5
-LOAD_AT = -6
-TURN_AT = -2
+LAG_NORMALISE = 3
+LAG_MIRROR = 4
+FIRST_STEP = -2
 PIECES_PER_STEP = 1
-FIRST_STEP = LOAD_AT
 LAST_STEP = len(UNITS) + LAG_MIRROR + 2 * HEADS // PIECE_HEADS // PIECES_PER_STEP + 4
 
 FLOPS = 2 * 2 * BATCH * HEADS * CHANNELS * CHANNELS * HEAD_TOKENS
@@ -48,7 +46,7 @@ def tile_channelgroupattention_pa_t_kernel(tc, qkv_bn, gra_sharp, out_0, out_1):
     nc = tc.nc
     with ExitStack() as stack:
         const = stack.enter_context(tc.tile_pool(name="const", bufs=1))
-        natural = stack.enter_context(tc.tile_pool(name="natural", bufs=1))
+        natural = stack.enter_context(tc.tile_pool(name="natural", bufs=2))
         turned = stack.enter_context(tc.tile_pool(name="turned", bufs=2))
         q_mx = stack.enter_context(tc.tile_pool(name="q_mx", bufs=2))
         stage = stack.enter_context(tc.tile_pool(name="stage", bufs=2))
@@ -79,6 +77,11 @@ def tile_channelgroupattention_pa_t_kernel(tc, qkv_bn, gra_sharp, out_0, out_1):
         banks, e, total, share = {}, {}, {}, {}
         row_fill, column_fill = {}, {}
 
+        def gpsimd_copy(out, in_):
+            nc.gpsimd.tensor_scalar(
+                out=out, in0=in_, scalar1=1.0, scalar2=0.0, op0=ALU.mult, op1=ALU.add
+            )
+
         def load_q(b):
             q_nat[b] = natural.tile([P, CT, TOKENS], BF16, name="q_nat")
             for t in range(CT):
@@ -96,19 +99,14 @@ def tile_channelgroupattention_pa_t_kernel(tc, qkv_bn, gra_sharp, out_0, out_1):
                         flipped[:, k, :], q_nat[b][:, t, m * P : (m + 1) * P], ident_bf[:]
                     )
                 target = q_t[b][:, 4 * g : 4 * g + 4, t * P : (t + 1) * P]
-                if g % 2 == 0:
-                    nc.scalar.copy(out=target, in_=flipped[:])
-                else:
-                    nc.vector.tensor_copy(out=target, in_=flipped[:])
+                nc.scalar.copy(out=target, in_=flipped[:])
 
         def regroup_q(b, piece):
             cols = slice(piece * Q_PIECE_TOKENS, (piece + 1) * Q_PIECE_TOKENS)
             q_grouped[b, piece] = stage.tile(
                 [P, Q_PIECE_TOKENS, CT], BF16, name="q_grouped", align_bytes=64
             )
-            nc.scalar.copy(
-                out=q_grouped[b, piece][:], in_=q_nat[b][:, :, cols].rearrange("p t w -> p w t")
-            )
+            gpsimd_copy(q_grouped[b, piece][:], q_nat[b][:, :, cols].rearrange("p t w -> p w t"))
 
         def quantise_q(b, piece):
             cols = slice(piece * Q_PIECE_TOKENS, (piece + 1) * Q_PIECE_TOKENS)
@@ -126,38 +124,34 @@ def tile_channelgroupattention_pa_t_kernel(tc, qkv_bn, gra_sharp, out_0, out_1):
             b, i, j = UNITS[u]
             banks[u] = []
             for half in range(BANKS):
-                bank = psum.tile([P, BANK_HEADS, P], F32, tag="scores", bufs=4)
-                for k in range(BANK_HEADS):
+                first = j * P + half * BANK_COLUMNS
+                bank = psum.tile([P, HEADS, BANK_COLUMNS], F32, tag="scores", bufs=4)
+                for n in range(HEADS):
                     for kt in range(KT):
-                        m = (half * BANK_HEADS + k) * KT + kt
                         nc.tensor.matmul(
-                            bank[:, k, :],
-                            lhsT=q_t[b][:, m, i * P : (i + 1) * P],
-                            rhs=q_t[b][:, m, j * P : (j + 1) * P],
+                            bank[:, n, :],
+                            lhsT=q_t[b][:, n * KT + kt, i * P : (i + 1) * P],
+                            rhs=q_t[b][:, n * KT + kt, first : first + BANK_COLUMNS],
                             start=(kt == 0),
                             stop=(kt == KT - 1),
                         )
                 banks[u].append(bank)
 
         def subtract_maximum(u):
-            bank_top = work.tile([P, BANKS, P], F32)
+            top = work.tile([P, BANKS, BANK_COLUMNS], F32)
             for half in range(BANKS):
                 nc.vector.tensor_reduce(
-                    out=bank_top[:, half, :],
+                    out=top[:, half, :],
                     in_=banks[u][half][:].rearrange("p n d -> p d n"),
                     axis=AXIS.X,
                     op=ALU.max,
                 )
-            top = work.tile([P, P], F32)
-            nc.vector.tensor_reduce(
-                out=top[:], in_=bank_top[:].rearrange("p h d -> p d h"), axis=AXIS.X, op=ALU.max
-            )
             e[u] = work.tile([P, HEADS, P], F32, name="e", bufs=LAG_NORMALISE + 1)
             for half in range(BANKS):
                 nc.vector.tensor_tensor(
-                    out=e[u][:, half * BANK_HEADS : (half + 1) * BANK_HEADS, :],
+                    out=e[u][:, :, half * BANK_COLUMNS : (half + 1) * BANK_COLUMNS],
                     in0=banks[u][half][:],
-                    in1=top[:].unsqueeze(1).to_broadcast([P, BANK_HEADS, P]),
+                    in1=top[:, half, :].unsqueeze(1).to_broadcast([P, HEADS, BANK_COLUMNS]),
                     op=ALU.subtract,
                 )
 
@@ -165,17 +159,9 @@ def tile_channelgroupattention_pa_t_kernel(tc, qkv_bn, gra_sharp, out_0, out_1):
             nc.scalar.activation(out=e[u][:], in_=e[u][:], func=ACT.Exp, scale=inv_sharp[:, 0:1])
 
         def sum_heads(u):
-            sum4 = work.tile([P, 4, P], F32)
-            nc.gpsimd.tensor_tensor(
-                out=sum4[:], in0=e[u][:, 0:4, :], in1=e[u][:, 4:8, :], op=ALU.add
-            )
-            sum2 = work.tile([P, 2, P], F32)
-            nc.gpsimd.tensor_tensor(
-                out=sum2[:], in0=sum4[:, 0:2, :], in1=sum4[:, 2:4, :], op=ALU.add
-            )
-            total[u] = work.tile([P, P], F32, name="total", bufs=3)
-            nc.gpsimd.tensor_tensor(
-                out=total[u][:], in0=sum2[:, 0, :], in1=sum2[:, 1, :], op=ALU.add
+            total[u] = work.tile([P, P], F32, name="total")
+            nc.vector.tensor_reduce(
+                out=total[u][:], in_=e[u][:].rearrange("p n d -> p d n"), axis=AXIS.X, op=ALU.add
             )
 
         def reciprocal(u):
@@ -233,7 +219,10 @@ def tile_channelgroupattention_pa_t_kernel(tc, qkv_bn, gra_sharp, out_0, out_1):
                 "p t n c -> p n c t"
             )
             a_grouped = a_mx.tile([P, PIECE_HEADS, P, CT], BF16, align_bytes=64)
-            nc.scalar.copy(out=a_grouped[:], in_=by_word)
+            if part == 0:
+                nc.scalar.copy(out=a_grouped[:], in_=by_word)
+            else:
+                gpsimd_copy(a_grouped[:], by_word)
             return piece, a_grouped
 
         def quantise(piece, a_grouped):
@@ -271,7 +260,7 @@ def tile_channelgroupattention_pa_t_kernel(tc, qkv_bn, gra_sharp, out_0, out_1):
             tiles = PIECE_HEADS * KT
             h_sb = h_pool.tile([P, tiles, P], F32)
             for half in range(tiles // 4):
-                nc.vector.tensor_copy(out=h_sb[:, half * 4 : (half + 1) * 4, :], in_=accs[half][:])
+                nc.scalar.copy(out=h_sb[:, half * 4 : (half + 1) * 4, :], in_=accs[half][:])
             h_rows = out_0[b].rearrange("(m w) c -> w m c", w=P)
             nc.sync.dma_start(
                 out=h_rows[:, part * tiles : (part + 1) * tiles, j * P : (j + 1) * P], in_=h_sb[:]
@@ -280,43 +269,39 @@ def tile_channelgroupattention_pa_t_kernel(tc, qkv_bn, gra_sharp, out_0, out_1):
         def is_unit(u):
             return 0 <= u < len(UNITS)
 
+        for b in range(BATCH):
+            load_q(b)
         waiting, regrouped, quantised, multiplied = [], [], [], []
         for step in range(FIRST_STEP, LAST_STEP):
-            if is_unit(step - LAG_MIRROR) and UNITS[step - LAG_MIRROR][1] != UNITS[step - LAG_MIRROR][2]:
-                mirror(step - LAG_MIRROR)
-            if is_unit(step + AHEAD_SCORES):
-                scores(step + AHEAD_SCORES)
-            if is_unit(step - LAG_RECIPROCAL):
-                reciprocal(step - LAG_RECIPROCAL)
             if is_unit(step - LAG_EXP):
                 exponential(step - LAG_EXP)
-            if is_unit(step - LAG_NORMALISE):
-                normalise(step - LAG_NORMALISE)
+            if is_unit(step + AHEAD_SCORES):
+                scores(step + AHEAD_SCORES)
             if is_unit(step - LAG_SUM):
                 sum_heads(step - LAG_SUM)
+            if is_unit(step - LAG_NORMALISE):
+                normalise(step - LAG_NORMALISE)
             for item in multiplied:
                 store_h(*item)
             if is_unit(step - LAG_MIRROR):
                 b, i, j = UNITS[step - LAG_MIRROR]
-                waiting.extend(block_written(b, i, j))
                 if i != j:
+                    mirror(step - LAG_MIRROR)
                     waiting.extend(block_written(b, j, i))
+                waiting.extend(block_written(b, i, j))
             multiplied = [multiply(*item) for item in quantised]
-            quantised = [quantise(*item) for item in regrouped]
+            to_quantise = regrouped
             regrouped = [regroup(piece) for piece in waiting[:PIECES_PER_STEP]]
             waiting = waiting[PIECES_PER_STEP:]
-            for b in range(BATCH):
-                since = step - b * BATCH_UNITS
-                if 0 <= since - 1 < Q_PIECES:
-                    quantise_q(b, since - 1)
-                if 0 <= since < Q_PIECES:
-                    regroup_q(b, since)
+            if 0 <= step < BATCH * Q_PIECES:
+                regroup_q(step // Q_PIECES, step % Q_PIECES)
             if is_unit(step):
                 subtract_maximum(step)
-            for b in range(BATCH):
-                since = step - b * BATCH_UNITS
-                if 0 <= since - TURN_AT < CT:
-                    turn_q(b, since - TURN_AT)
-                if since == LOAD_AT:
-                    load_q(b)
+            if is_unit(step - LAG_SUM):
+                reciprocal(step - LAG_SUM)
+            quantised = [quantise(*item) for item in to_quantise]
+            if 0 <= step - 1 < BATCH * Q_PIECES:
+                quantise_q((step - 1) // Q_PIECES, (step - 1) % Q_PIECES)
+            if step - FIRST_STEP < BATCH * CT:
+                turn_q((step - FIRST_STEP) // CT, (step - FIRST_STEP) % CT)
         assert not (waiting or regrouped or quantised or multiplied)

@@ -146,12 +146,12 @@ def tile_channelgroupattention_pa_t_kernel(tc, qkv_bn, gra_sharp, out_0, out_1):
                     axis=AXIS.X,
                     op=ALU.max,
                 )
-            e[u] = work.tile([P, HEADS, P], F32, name="e", bufs=LAG_NORMALISE + 1)
+            e[u] = work.tile([P, P, HEADS], F32, name="e", bufs=LAG_NORMALISE + 1)
             for half in range(BANKS):
                 nc.vector.tensor_tensor(
-                    out=e[u][:, :, half * BANK_COLUMNS : (half + 1) * BANK_COLUMNS],
-                    in0=banks[u][half][:],
-                    in1=top[:, half, :].unsqueeze(1).to_broadcast([P, HEADS, BANK_COLUMNS]),
+                    out=e[u][:, half * BANK_COLUMNS : (half + 1) * BANK_COLUMNS, :],
+                    in0=banks[u][half][:].rearrange("p n d -> p d n"),
+                    in1=top[:, half, :].unsqueeze(2).to_broadcast([P, BANK_COLUMNS, HEADS]),
                     op=ALU.subtract,
                 )
 
@@ -161,7 +161,7 @@ def tile_channelgroupattention_pa_t_kernel(tc, qkv_bn, gra_sharp, out_0, out_1):
         def sum_heads(u):
             total[u] = work.tile([P, P], F32, name="total")
             nc.vector.tensor_reduce(
-                out=total[u][:], in_=e[u][:].rearrange("p n d -> p d n"), axis=AXIS.X, op=ALU.add
+                out=total[u][:], in_=e[u][:], axis=AXIS.X, op=ALU.add
             )
 
         def reciprocal(u):
@@ -179,7 +179,7 @@ def tile_channelgroupattention_pa_t_kernel(tc, qkv_bn, gra_sharp, out_0, out_1):
                 column_fill[b] = [0] * CT
             nc.gpsimd.tensor_tensor(
                 out=block_of(b, i, j),
-                in0=e[u][:],
+                in0=e[u][:].rearrange("p d n -> p n d"),
                 in1=share[u][:].unsqueeze(1).to_broadcast([P, HEADS, P]),
                 op=ALU.mult,
             )

@@ -24,7 +24,7 @@ BANK_COLUMNS = P // BANKS
 PANEL_TILES = 2
 PANELS = CT // PANEL_TILES
 PIECE_HEADS = 4
-Q_PIECES = 4
+Q_PIECES = 2
 Q_PIECE_TOKENS = TOKENS // Q_PIECES
 
 UNITS = [(b, i, j) for b in range(BATCH) for i in range(CT) for j in range(i, CT)]
@@ -35,9 +35,12 @@ LAG_EXP = 1
 LAG_SUM = 2
 LAG_NORMALISE = 3
 LAG_MIRROR = 4
-FIRST_STEP = -2
-PIECES_PER_STEP = 1
-LAST_STEP = len(UNITS) + LAG_MIRROR + 2 * HEADS // PIECE_HEADS // PIECES_PER_STEP + 4
+Q_STAGGER = 6
+LOAD_AT = -4
+TURN_AT = -2
+REGROUP_AT = 0
+FIRST_STEP = LOAD_AT
+LAST_STEP = len(UNITS) + LAG_MIRROR + 10
 
 FLOPS = 2 * 2 * BATCH * HEADS * CHANNELS * CHANNELS * HEAD_TOKENS
 
@@ -46,10 +49,10 @@ def tile_channelgroupattention_pa_t_kernel(tc, qkv_bn, gra_sharp, out_0, out_1):
     nc = tc.nc
     with ExitStack() as stack:
         const = stack.enter_context(tc.tile_pool(name="const", bufs=1))
-        natural = stack.enter_context(tc.tile_pool(name="natural", bufs=2))
+        natural = stack.enter_context(tc.tile_pool(name="natural", bufs=1))
         turned = stack.enter_context(tc.tile_pool(name="turned", bufs=2))
         q_mx = stack.enter_context(tc.tile_pool(name="q_mx", bufs=2))
-        stage = stack.enter_context(tc.tile_pool(name="stage", bufs=2))
+        stage = stack.enter_context(tc.tile_pool(name="stage", bufs=1))
         panels = stack.enter_context(tc.tile_pool(name="panels", bufs=3))
         work = stack.enter_context(tc.tile_pool(name="work", bufs=2))
         a_mx = stack.enter_context(tc.tile_pool(name="a_mx", bufs=2))
@@ -106,7 +109,10 @@ def tile_channelgroupattention_pa_t_kernel(tc, qkv_bn, gra_sharp, out_0, out_1):
             q_grouped[b, piece] = stage.tile(
                 [P, Q_PIECE_TOKENS, CT], BF16, name="q_grouped", align_bytes=64
             )
-            gpsimd_copy(q_grouped[b, piece][:], q_nat[b][:, :, cols].rearrange("p t w -> p w t"))
+            by_word = q_nat[b][:, :, cols].rearrange("p t w -> p w t")
+            half = Q_PIECE_TOKENS // 2
+            gpsimd_copy(q_grouped[b, piece][:, :half], by_word[:, :half])
+            gpsimd_copy(q_grouped[b, piece][:, half:], by_word[:, half:])
 
         def quantise_q(b, piece):
             cols = slice(piece * Q_PIECE_TOKENS, (piece + 1) * Q_PIECE_TOKENS)
@@ -208,32 +214,28 @@ def tile_channelgroupattention_pa_t_kernel(tc, qkv_bn, gra_sharp, out_0, out_1):
                 )
             column_fill[b][j] += 1
             if column_fill[b][j] == CT:
-                return [(b, j, part) for part in range(HEADS // PIECE_HEADS)]
+                return [(b, j)]
             return []
 
-        def regroup(piece):
-            b, j, part = piece
+        def regroup(b, j):
             first = (j % PANEL_TILES) * P
-            heads = slice(part * PIECE_HEADS, (part + 1) * PIECE_HEADS)
-            by_word = panel[b][j // PANEL_TILES][:, :, heads, first : first + P].rearrange(
+            by_word = panel[b][j // PANEL_TILES][:, :, :, first : first + P].rearrange(
                 "p t n c -> p n c t"
             )
-            a_grouped = a_mx.tile([P, PIECE_HEADS, P, CT], BF16, align_bytes=64)
-            if part == 0:
-                nc.scalar.copy(out=a_grouped[:], in_=by_word)
-            else:
-                gpsimd_copy(a_grouped[:], by_word)
-            return piece, a_grouped
+            a_grouped = a_mx.tile([P, HEADS, P, CT], BF16, align_bytes=64)
+            nc.scalar.copy(out=a_grouped[:, :PIECE_HEADS], in_=by_word[:, :PIECE_HEADS])
+            gpsimd_copy(a_grouped[:, PIECE_HEADS:], by_word[:, PIECE_HEADS:])
+            return b, j, a_grouped
 
-        def quantise(piece, a_grouped):
-            a_codes = a_mx.tile([P, PIECE_HEADS * P], U32, align_bytes=64)
-            a_scales = a_mx.tile([P, PIECE_HEADS * P], U8, align_bytes=64)
+        def quantise(b, j, a_grouped):
+            a_codes = a_mx.tile([P, HEADS * P], U32, align_bytes=64)
+            a_scales = a_mx.tile([P, HEADS * P], U8, align_bytes=64)
             nc.vector.quantize_mx(
                 out=a_codes[:].bitcast(FP8X4),
                 scales=a_scales[:],
                 in_=a_grouped[:].rearrange("p n c t -> p (n c t)"),
             )
-            return piece, a_codes, a_scales
+            return [((b, j, part), a_codes, a_scales) for part in range(HEADS // PIECE_HEADS)]
 
         def multiply(piece, a_codes, a_scales):
             b, j, part = piece
@@ -241,7 +243,7 @@ def tile_channelgroupattention_pa_t_kernel(tc, qkv_bn, gra_sharp, out_0, out_1):
             for half in range(PIECE_HEADS * KT // 4):
                 acc = psum.tile([P, 4, P], F32, tag="acc")
                 for k in range(4):
-                    n = (half * 4 + k) // KT
+                    n = part * PIECE_HEADS + (half * 4 + k) // KT
                     m = part * PIECE_HEADS * KT + half * 4 + k
                     nc.tensor.matmul_mx(
                         out=acc[:, k, :],
@@ -269,8 +271,6 @@ def tile_channelgroupattention_pa_t_kernel(tc, qkv_bn, gra_sharp, out_0, out_1):
         def is_unit(u):
             return 0 <= u < len(UNITS)
 
-        for b in range(BATCH):
-            load_q(b)
         waiting, regrouped, quantised, multiplied = [], [], [], []
         for step in range(FIRST_STEP, LAST_STEP):
             if is_unit(step - LAG_EXP):
@@ -289,19 +289,28 @@ def tile_channelgroupattention_pa_t_kernel(tc, qkv_bn, gra_sharp, out_0, out_1):
                     mirror(step - LAG_MIRROR)
                     waiting.extend(block_written(b, j, i))
                 waiting.extend(block_written(b, i, j))
-            multiplied = [multiply(*item) for item in quantised]
+            multiplied = [multiply(*item) for item in quantised[:1]]
+            quantised = quantised[1:]
             to_quantise = regrouped
-            regrouped = [regroup(piece) for piece in waiting[:PIECES_PER_STEP]]
-            waiting = waiting[PIECES_PER_STEP:]
-            if 0 <= step < BATCH * Q_PIECES:
-                regroup_q(step // Q_PIECES, step % Q_PIECES)
+            regrouped = [regroup(*column) for column in waiting[:1]]
+            waiting = waiting[1:]
+            for b in range(BATCH):
+                turn = step - Q_STAGGER * b - REGROUP_AT
+                if 0 <= turn < 2 * Q_PIECES and turn % 2 == 0:
+                    regroup_q(b, turn // 2)
             if is_unit(step):
                 subtract_maximum(step)
             if is_unit(step - LAG_SUM):
                 reciprocal(step - LAG_SUM)
-            quantised = [quantise(*item) for item in to_quantise]
-            if 0 <= step - 1 < BATCH * Q_PIECES:
-                quantise_q((step - 1) // Q_PIECES, (step - 1) % Q_PIECES)
-            if step - FIRST_STEP < BATCH * CT:
-                turn_q((step - FIRST_STEP) // CT, (step - FIRST_STEP) % CT)
+            for item in to_quantise:
+                quantised.extend(quantise(*item))
+            for b in range(BATCH):
+                since = step - Q_STAGGER * b
+                turn = since - REGROUP_AT
+                if 0 <= turn < 2 * Q_PIECES and turn % 2 == 1:
+                    quantise_q(b, turn // 2)
+                if 0 <= since - TURN_AT < CT:
+                    turn_q(b, since - TURN_AT)
+                if since == LOAD_AT:
+                    load_q(b)
         assert not (waiting or regrouped or quantised or multiplied)

@@ -24,7 +24,7 @@ BANK_COLUMNS = P // BANKS
 PANEL_TILES = 2
 PANELS = CT // PANEL_TILES
 PIECE_HEADS = 4
-Q_PIECES = 2
+Q_PIECES = 4
 Q_PIECE_TOKENS = TOKENS // Q_PIECES
 
 UNITS = [(b, i, j) for b in range(BATCH) for i in range(CT) for j in range(i, CT)]
@@ -34,13 +34,11 @@ AHEAD_SCORES = 1
 LAG_EXP = 1
 LAG_SUM = 2
 LAG_NORMALISE = 3
-LAG_MIRROR = 4
-Q_STAGGER = 6
-LOAD_AT = -4
-TURN_AT = -2
-REGROUP_AT = 0
-FIRST_STEP = LOAD_AT
-LAST_STEP = len(UNITS) + LAG_MIRROR + 10
+LAG_MIRROR = 5
+E_BUFFERS = LAG_NORMALISE + 2
+FIRST_STEP = -2
+PIECES_PER_STEP = 1
+LAST_STEP = len(UNITS) + LAG_MIRROR + 2 * HEADS // PIECE_HEADS // PIECES_PER_STEP + 4
 
 FLOPS = 2 * 2 * BATCH * HEADS * CHANNELS * CHANNELS * HEAD_TOKENS
 
@@ -49,10 +47,10 @@ def tile_channelgroupattention_pa_t_kernel(tc, qkv_bn, gra_sharp, out_0, out_1):
     nc = tc.nc
     with ExitStack() as stack:
         const = stack.enter_context(tc.tile_pool(name="const", bufs=1))
-        natural = stack.enter_context(tc.tile_pool(name="natural", bufs=1))
+        natural = stack.enter_context(tc.tile_pool(name="natural", bufs=2))
         turned = stack.enter_context(tc.tile_pool(name="turned", bufs=2))
         q_mx = stack.enter_context(tc.tile_pool(name="q_mx", bufs=2))
-        stage = stack.enter_context(tc.tile_pool(name="stage", bufs=1))
+        stage = stack.enter_context(tc.tile_pool(name="stage", bufs=2))
         panels = stack.enter_context(tc.tile_pool(name="panels", bufs=3))
         work = stack.enter_context(tc.tile_pool(name="work", bufs=2))
         a_mx = stack.enter_context(tc.tile_pool(name="a_mx", bufs=2))
@@ -110,9 +108,10 @@ def tile_channelgroupattention_pa_t_kernel(tc, qkv_bn, gra_sharp, out_0, out_1):
                 [P, Q_PIECE_TOKENS, CT], BF16, name="q_grouped", align_bytes=64
             )
             by_word = q_nat[b][:, :, cols].rearrange("p t w -> p w t")
-            half = Q_PIECE_TOKENS // 2
-            gpsimd_copy(q_grouped[b, piece][:, :half], by_word[:, :half])
-            gpsimd_copy(q_grouped[b, piece][:, half:], by_word[:, half:])
+            if b == 0:
+                gpsimd_copy(q_grouped[b, piece][:], by_word)
+            else:
+                nc.scalar.copy(out=q_grouped[b, piece][:], in_=by_word)
 
         def quantise_q(b, piece):
             cols = slice(piece * Q_PIECE_TOKENS, (piece + 1) * Q_PIECE_TOKENS)
@@ -152,7 +151,7 @@ def tile_channelgroupattention_pa_t_kernel(tc, qkv_bn, gra_sharp, out_0, out_1):
                     axis=AXIS.X,
                     op=ALU.max,
                 )
-            e[u] = work.tile([P, P, HEADS], F32, name="e", bufs=LAG_NORMALISE + 1)
+            e[u] = work.tile([P, P, HEADS], F32, name="e", bufs=E_BUFFERS)
             for half in range(BANKS):
                 nc.vector.tensor_tensor(
                     out=e[u][:, half * BANK_COLUMNS : (half + 1) * BANK_COLUMNS, :],
@@ -214,28 +213,32 @@ def tile_channelgroupattention_pa_t_kernel(tc, qkv_bn, gra_sharp, out_0, out_1):
                 )
             column_fill[b][j] += 1
             if column_fill[b][j] == CT:
-                return [(b, j)]
+                return [(b, j, part) for part in range(HEADS // PIECE_HEADS)]
             return []
 
-        def regroup(b, j):
+        def regroup(piece):
+            b, j, part = piece
             first = (j % PANEL_TILES) * P
-            by_word = panel[b][j // PANEL_TILES][:, :, :, first : first + P].rearrange(
+            heads = slice(part * PIECE_HEADS, (part + 1) * PIECE_HEADS)
+            by_word = panel[b][j // PANEL_TILES][:, :, heads, first : first + P].rearrange(
                 "p t n c -> p n c t"
             )
-            a_grouped = a_mx.tile([P, HEADS, P, CT], BF16, align_bytes=64)
-            nc.scalar.copy(out=a_grouped[:, :PIECE_HEADS], in_=by_word[:, :PIECE_HEADS])
-            gpsimd_copy(a_grouped[:, PIECE_HEADS:], by_word[:, PIECE_HEADS:])
-            return b, j, a_grouped
+            a_grouped = a_mx.tile([P, PIECE_HEADS, P, CT], BF16, align_bytes=64)
+            if part == 0:
+                nc.scalar.copy(out=a_grouped[:], in_=by_word)
+            else:
+                gpsimd_copy(a_grouped[:], by_word)
+            return piece, a_grouped
 
-        def quantise(b, j, a_grouped):
-            a_codes = a_mx.tile([P, HEADS * P], U32, align_bytes=64)
-            a_scales = a_mx.tile([P, HEADS * P], U8, align_bytes=64)
+        def quantise(piece, a_grouped):
+            a_codes = a_mx.tile([P, PIECE_HEADS * P], U32, align_bytes=64)
+            a_scales = a_mx.tile([P, PIECE_HEADS * P], U8, align_bytes=64)
             nc.vector.quantize_mx(
                 out=a_codes[:].bitcast(FP8X4),
                 scales=a_scales[:],
                 in_=a_grouped[:].rearrange("p n c t -> p (n c t)"),
             )
-            return [((b, j, part), a_codes, a_scales) for part in range(HEADS // PIECE_HEADS)]
+            return piece, a_codes, a_scales
 
         def multiply(piece, a_codes, a_scales):
             b, j, part = piece
@@ -243,7 +246,7 @@ def tile_channelgroupattention_pa_t_kernel(tc, qkv_bn, gra_sharp, out_0, out_1):
             for half in range(PIECE_HEADS * KT // 4):
                 acc = psum.tile([P, 4, P], F32, tag="acc")
                 for k in range(4):
-                    n = part * PIECE_HEADS + (half * 4 + k) // KT
+                    n = (half * 4 + k) // KT
                     m = part * PIECE_HEADS * KT + half * 4 + k
                     nc.tensor.matmul_mx(
                         out=acc[:, k, :],
@@ -271,6 +274,8 @@ def tile_channelgroupattention_pa_t_kernel(tc, qkv_bn, gra_sharp, out_0, out_1):
         def is_unit(u):
             return 0 <= u < len(UNITS)
 
+        for b in range(BATCH):
+            load_q(b)
         waiting, regrouped, quantised, multiplied = [], [], [], []
         for step in range(FIRST_STEP, LAST_STEP):
             if is_unit(step - LAG_EXP):
@@ -289,28 +294,19 @@ def tile_channelgroupattention_pa_t_kernel(tc, qkv_bn, gra_sharp, out_0, out_1):
                     mirror(step - LAG_MIRROR)
                     waiting.extend(block_written(b, j, i))
                 waiting.extend(block_written(b, i, j))
-            multiplied = [multiply(*item) for item in quantised[:1]]
-            quantised = quantised[1:]
+            multiplied = [multiply(*item) for item in quantised]
             to_quantise = regrouped
-            regrouped = [regroup(*column) for column in waiting[:1]]
-            waiting = waiting[1:]
-            for b in range(BATCH):
-                turn = step - Q_STAGGER * b - REGROUP_AT
-                if 0 <= turn < 2 * Q_PIECES and turn % 2 == 0:
-                    regroup_q(b, turn // 2)
+            regrouped = [regroup(piece) for piece in waiting[:PIECES_PER_STEP]]
+            waiting = waiting[PIECES_PER_STEP:]
+            if 0 <= step < BATCH * Q_PIECES:
+                regroup_q(step // Q_PIECES, step % Q_PIECES)
             if is_unit(step):
                 subtract_maximum(step)
             if is_unit(step - LAG_SUM):
                 reciprocal(step - LAG_SUM)
-            for item in to_quantise:
-                quantised.extend(quantise(*item))
-            for b in range(BATCH):
-                since = step - Q_STAGGER * b
-                turn = since - REGROUP_AT
-                if 0 <= turn < 2 * Q_PIECES and turn % 2 == 1:
-                    quantise_q(b, turn // 2)
-                if 0 <= since - TURN_AT < CT:
-                    turn_q(b, since - TURN_AT)
-                if since == LOAD_AT:
-                    load_q(b)
+            quantised = [quantise(*item) for item in to_quantise]
+            if 0 <= step - 1 < BATCH * Q_PIECES:
+                quantise_q((step - 1) // Q_PIECES, (step - 1) % Q_PIECES)
+            if step - FIRST_STEP < BATCH * CT:
+                turn_q((step - FIRST_STEP) // CT, (step - FIRST_STEP) % CT)
         assert not (waiting or regrouped or quantised or multiplied)

@@ -33,8 +33,8 @@ BATCH_UNITS = len(UNITS) // BATCH
 AHEAD_SCORES = 1
 LAG_EXP = 1
 LAG_SUM = 2
-LAG_NORMALISE = 3
-LAG_MIRROR = 5
+LAG_NORMALISE = 2
+LAG_MIRROR = 4
 E_BUFFERS = LAG_NORMALISE + 2
 FIRST_STEP = -2
 PIECES_PER_STEP = 1
@@ -93,7 +93,7 @@ def tile_channelgroupattention_pa_t_kernel(tc, qkv_bn, gra_sharp, out_0, out_1):
 
         def turn_q(b, t):
             for g in range(TOKEN_TILES // 4):
-                flipped = psum.tile([P, 4, P], BF16, tag="flip")
+                flipped = psum.tile([P, 4, P], BF16, tag="flip", bufs=3)
                 for k in range(4):
                     m = 4 * g + k
                     nc.tensor.transpose(
@@ -108,10 +108,7 @@ def tile_channelgroupattention_pa_t_kernel(tc, qkv_bn, gra_sharp, out_0, out_1):
                 [P, Q_PIECE_TOKENS, CT], BF16, name="q_grouped", align_bytes=64
             )
             by_word = q_nat[b][:, :, cols].rearrange("p t w -> p w t")
-            if b == 0:
-                gpsimd_copy(q_grouped[b, piece][:], by_word)
-            else:
-                nc.scalar.copy(out=q_grouped[b, piece][:], in_=by_word)
+            gpsimd_copy(q_grouped[b, piece][:], by_word)
 
         def quantise_q(b, piece):
             cols = slice(piece * Q_PIECE_TOKENS, (piece + 1) * Q_PIECE_TOKENS)
@@ -151,12 +148,12 @@ def tile_channelgroupattention_pa_t_kernel(tc, qkv_bn, gra_sharp, out_0, out_1):
                     axis=AXIS.X,
                     op=ALU.max,
                 )
-            e[u] = work.tile([P, P, HEADS], F32, name="e", bufs=E_BUFFERS)
+            e[u] = work.tile([P, HEADS, P], F32, name="e", bufs=E_BUFFERS)
             for half in range(BANKS):
                 nc.vector.tensor_tensor(
-                    out=e[u][:, half * BANK_COLUMNS : (half + 1) * BANK_COLUMNS, :],
-                    in0=banks[u][half][:].rearrange("p n d -> p d n"),
-                    in1=top[:, half, :].unsqueeze(2).to_broadcast([P, BANK_COLUMNS, HEADS]),
+                    out=e[u][:, :, half * BANK_COLUMNS : (half + 1) * BANK_COLUMNS],
+                    in0=banks[u][half][:],
+                    in1=top[:, half, :].unsqueeze(1).to_broadcast([P, HEADS, BANK_COLUMNS]),
                     op=ALU.subtract,
                 )
 
@@ -164,10 +161,15 @@ def tile_channelgroupattention_pa_t_kernel(tc, qkv_bn, gra_sharp, out_0, out_1):
             nc.scalar.activation(out=e[u][:], in_=e[u][:], func=ACT.Exp, scale=inv_sharp[:, 0:1])
 
         def sum_heads(u):
-            total[u] = work.tile([P, P], F32, name="total")
-            nc.vector.tensor_reduce(
-                out=total[u][:], in_=e[u][:], axis=AXIS.X, op=ALU.add
-            )
+            total[u] = psum.tile([P, P], F32, name="total", tag="total", bufs=1)
+            for n in range(HEADS):
+                nc.tensor.matmul(
+                    total[u][:],
+                    lhsT=ident_f32[:],
+                    rhs=e[u][:, n, :],
+                    start=(n == 0),
+                    stop=(n == HEADS - 1),
+                )
 
         def reciprocal(u):
             share[u] = work.tile([P, P], F32, name="share", bufs=3)
@@ -184,7 +186,7 @@ def tile_channelgroupattention_pa_t_kernel(tc, qkv_bn, gra_sharp, out_0, out_1):
                 column_fill[b] = [0] * CT
             nc.gpsimd.tensor_tensor(
                 out=block_of(b, i, j),
-                in0=e[u][:].rearrange("p d n -> p n d"),
+                in0=e[u][:],
                 in1=share[u][:].unsqueeze(1).to_broadcast([P, HEADS, P]),
                 op=ALU.mult,
             )
@@ -193,7 +195,7 @@ def tile_channelgroupattention_pa_t_kernel(tc, qkv_bn, gra_sharp, out_0, out_1):
             b, i, j = UNITS[u]
             for half in range(BANKS):
                 heads = slice(half * BANK_HEADS, (half + 1) * BANK_HEADS)
-                flipped = psum.tile([P, BANK_HEADS, P], F32, tag="flip")
+                flipped = psum.tile([P, BANK_HEADS, P], F32, tag="flip", bufs=3)
                 for k in range(BANK_HEADS):
                     nc.tensor.transpose(
                         flipped[:, k, :],
@@ -227,7 +229,7 @@ def tile_channelgroupattention_pa_t_kernel(tc, qkv_bn, gra_sharp, out_0, out_1):
             if part == 0:
                 nc.scalar.copy(out=a_grouped[:], in_=by_word)
             else:
-                gpsimd_copy(a_grouped[:], by_word)
+                nc.vector.tensor_copy(out=a_grouped[:], in_=by_word)
             return piece, a_grouped
 
         def quantise(piece, a_grouped):
@@ -244,7 +246,7 @@ def tile_channelgroupattention_pa_t_kernel(tc, qkv_bn, gra_sharp, out_0, out_1):
             b, j, part = piece
             accs = []
             for half in range(PIECE_HEADS * KT // 4):
-                acc = psum.tile([P, 4, P], F32, tag="acc")
+                acc = psum.tile([P, 4, P], F32, tag="flip", bufs=3)
                 for k in range(4):
                     n = (half * 4 + k) // KT
                     m = part * PIECE_HEADS * KT + half * 4 + k
@@ -284,8 +286,6 @@ def tile_channelgroupattention_pa_t_kernel(tc, qkv_bn, gra_sharp, out_0, out_1):
                 scores(step + AHEAD_SCORES)
             if is_unit(step - LAG_SUM):
                 sum_heads(step - LAG_SUM)
-            if is_unit(step - LAG_NORMALISE):
-                normalise(step - LAG_NORMALISE)
             for item in multiplied:
                 store_h(*item)
             if is_unit(step - LAG_MIRROR):
@@ -296,17 +296,19 @@ def tile_channelgroupattention_pa_t_kernel(tc, qkv_bn, gra_sharp, out_0, out_1):
                 waiting.extend(block_written(b, i, j))
             multiplied = [multiply(*item) for item in quantised]
             to_quantise = regrouped
-            regrouped = [regroup(piece) for piece in waiting[:PIECES_PER_STEP]]
-            waiting = waiting[PIECES_PER_STEP:]
             if 0 <= step < BATCH * Q_PIECES:
                 regroup_q(step // Q_PIECES, step % Q_PIECES)
             if is_unit(step):
                 subtract_maximum(step)
-            if is_unit(step - LAG_SUM):
-                reciprocal(step - LAG_SUM)
+            regrouped = [regroup(piece) for piece in waiting[:PIECES_PER_STEP]]
+            waiting = waiting[PIECES_PER_STEP:]
             quantised = [quantise(*item) for item in to_quantise]
             if 0 <= step - 1 < BATCH * Q_PIECES:
                 quantise_q((step - 1) // Q_PIECES, (step - 1) % Q_PIECES)
+            if is_unit(step - LAG_SUM):
+                reciprocal(step - LAG_SUM)
+            if is_unit(step - LAG_NORMALISE):
+                normalise(step - LAG_NORMALISE)
             if step - FIRST_STEP < BATCH * CT:
                 turn_q((step - FIRST_STEP) // CT, (step - FIRST_STEP) % CT)
         assert not (waiting or regrouped or quantised or multiplied)

@@ -30,15 +30,22 @@ Q_PIECE_TOKENS = TOKENS // Q_PIECES
 UNITS = [(b, i, j) for b in range(BATCH) for i in range(CT) for j in range(i, CT)]
 BATCH_UNITS = len(UNITS) // BATCH
 
-AHEAD_SCORES = 1
-LAG_EXP = 1
-LAG_SUM = 2
-LAG_NORMALISE = 2
-LAG_MIRROR = 4
-E_BUFFERS = LAG_NORMALISE + 2
-FIRST_STEP = -2
-PIECES_PER_STEP = 1
-LAST_STEP = len(UNITS) + LAG_MIRROR + 2 * HEADS // PIECE_HEADS // PIECES_PER_STEP + 4
+SCORES = -0.9
+EXPONENTIAL = 0.4
+SUM_TENSOR = 1.0
+SUM_VECTOR = 1.4
+RECIPROCAL = 1.7
+NORMALISE = 1.7
+MIRROR = 2.6
+REGROUP = 3.0
+REGROUP_LAST = 3.2
+NEXT_PIECE = 0.9
+QUANTISE = 1.1
+MULTIPLY = 1.8
+E_BUFFERS = 4
+TURN_FIRST = (-1.0, 2.0)
+Q_REGROUP_FIRST = (0.0, 6.0)
+Q_QUANTISE = 1.75
 
 FLOPS = 2 * 2 * BATCH * HEADS * CHANNELS * CHANNELS * HEAD_TOKENS
 
@@ -54,7 +61,7 @@ def tile_channelgroupattention_pa_t_kernel(tc, qkv_bn, gra_sharp, out_0, out_1):
         panels = stack.enter_context(tc.tile_pool(name="panels", bufs=3))
         work = stack.enter_context(tc.tile_pool(name="work", bufs=2))
         a_mx = stack.enter_context(tc.tile_pool(name="a_mx", bufs=2))
-        h_pool = stack.enter_context(tc.tile_pool(name="h_pool", bufs=2))
+        h_pool = stack.enter_context(tc.tile_pool(name="h_pool", bufs=4))
         psum = stack.enter_context(tc.psum_pool(name="psum", bufs=2))
         stack.enter_context(tc.manual_schedule())
 
@@ -75,13 +82,27 @@ def tile_channelgroupattention_pa_t_kernel(tc, qkv_bn, gra_sharp, out_0, out_1):
         nc.scalar.activation(out=warm[:], in_=warm[:], func=ACT.Exp)
 
         q_nat, q_t, q_grouped, q_codes, q_scales, panel = {}, {}, {}, {}, {}, {}
-        banks, e, total, share = {}, {}, {}, {}
-        row_fill, column_fill = {}, {}
+        banks, e, by_head, total, share = {}, {}, {}, {}, {}
+        row_fill, pieces = {}, {}
 
         def gpsimd_copy(out, in_):
             nc.gpsimd.tensor_scalar(
                 out=out, in0=in_, scalar1=1.0, scalar2=0.0, op0=ALU.mult, op1=ALU.add
             )
+
+        def copy_words(engine, words, by_word):
+            if len(words.shape) == 3:
+                out = words.rearrange("p (c i) t -> p c t i", i=4)
+                in_ = by_word.rearrange("p (c i) t -> p c t i", i=4)
+            else:
+                out = words.rearrange("p n (c i) t -> p n c t i", i=4)
+                in_ = by_word.rearrange("p n (c i) t -> p n c t i", i=4)
+            if engine == "scalar":
+                nc.scalar.copy(out=out, in_=in_)
+            elif engine == "vector":
+                nc.vector.tensor_copy(out=out, in_=in_)
+            else:
+                gpsimd_copy(out, in_)
 
         def load_q(b):
             q_nat[b] = natural.tile([P, CT, TOKENS], BF16, name="q_nat")
@@ -108,7 +129,7 @@ def tile_channelgroupattention_pa_t_kernel(tc, qkv_bn, gra_sharp, out_0, out_1):
                 [P, Q_PIECE_TOKENS, CT], BF16, name="q_grouped", align_bytes=64
             )
             by_word = q_nat[b][:, :, cols].rearrange("p t w -> p w t")
-            gpsimd_copy(q_grouped[b, piece][:], by_word)
+            copy_words("gpsimd", q_grouped[b, piece][:], by_word)
 
         def quantise_q(b, piece):
             cols = slice(piece * Q_PIECE_TOKENS, (piece + 1) * Q_PIECE_TOKENS)
@@ -139,6 +160,9 @@ def tile_channelgroupattention_pa_t_kernel(tc, qkv_bn, gra_sharp, out_0, out_1):
                         )
                 banks[u].append(bank)
 
+        def summed_on_tensor(u):
+            return u % 3 != 1
+
         def subtract_maximum(u):
             top = work.tile([P, BANKS, BANK_COLUMNS], F32)
             for half in range(BANKS):
@@ -148,28 +172,46 @@ def tile_channelgroupattention_pa_t_kernel(tc, qkv_bn, gra_sharp, out_0, out_1):
                     axis=AXIS.X,
                     op=ALU.max,
                 )
-            e[u] = work.tile([P, HEADS, P], F32, name="e", bufs=E_BUFFERS)
+            if summed_on_tensor(u):
+                e[u] = work.tile([P, HEADS, P], F32, name="e", tag="e", bufs=E_BUFFERS)
+                by_head[u] = e[u][:]
+            else:
+                e[u] = work.tile([P, P, HEADS], F32, name="e", tag="e", bufs=E_BUFFERS)
+                by_head[u] = e[u][:].rearrange("p d n -> p n d")
             for half in range(BANKS):
-                nc.vector.tensor_tensor(
-                    out=e[u][:, :, half * BANK_COLUMNS : (half + 1) * BANK_COLUMNS],
-                    in0=banks[u][half][:],
-                    in1=top[:, half, :].unsqueeze(1).to_broadcast([P, HEADS, BANK_COLUMNS]),
-                    op=ALU.subtract,
-                )
+                columns = slice(half * BANK_COLUMNS, (half + 1) * BANK_COLUMNS)
+                if summed_on_tensor(u):
+                    nc.vector.tensor_tensor(
+                        out=e[u][:, :, columns],
+                        in0=banks[u][half][:],
+                        in1=top[:, half, :].unsqueeze(1).to_broadcast([P, HEADS, BANK_COLUMNS]),
+                        op=ALU.subtract,
+                    )
+                else:
+                    nc.vector.tensor_tensor(
+                        out=e[u][:, columns, :],
+                        in0=banks[u][half][:].rearrange("p n d -> p d n"),
+                        in1=top[:, half, :].unsqueeze(2).to_broadcast([P, BANK_COLUMNS, HEADS]),
+                        op=ALU.subtract,
+                    )
 
         def exponential(u):
             nc.scalar.activation(out=e[u][:], in_=e[u][:], func=ACT.Exp, scale=inv_sharp[:, 0:1])
 
         def sum_heads(u):
-            total[u] = psum.tile([P, P], F32, name="total", tag="total", bufs=1)
-            for n in range(HEADS):
-                nc.tensor.matmul(
-                    total[u][:],
-                    lhsT=ident_f32[:],
-                    rhs=e[u][:, n, :],
-                    start=(n == 0),
-                    stop=(n == HEADS - 1),
-                )
+            if summed_on_tensor(u):
+                total[u] = psum.tile([P, P], F32, name="total_t", tag="total", bufs=1)
+                for n in range(HEADS):
+                    nc.tensor.matmul(
+                        total[u][:],
+                        lhsT=ident_f32[:],
+                        rhs=e[u][:, n, :],
+                        start=(n == 0),
+                        stop=(n == HEADS - 1),
+                    )
+            else:
+                total[u] = work.tile([P, P], F32, name="total_v")
+                nc.vector.tensor_reduce(out=total[u][:], in_=e[u][:], axis=AXIS.X, op=ALU.add)
 
         def reciprocal(u):
             share[u] = work.tile([P, P], F32, name="share", bufs=3)
@@ -183,13 +225,16 @@ def tile_channelgroupattention_pa_t_kernel(tc, qkv_bn, gra_sharp, out_0, out_1):
                     for J in range(PANELS)
                 ]
                 row_fill[b] = [[0] * CT for J in range(PANELS)]
-                column_fill[b] = [0] * CT
-            nc.gpsimd.tensor_tensor(
-                out=block_of(b, i, j),
-                in0=e[u][:],
-                in1=share[u][:].unsqueeze(1).to_broadcast([P, HEADS, P]),
-                op=ALU.mult,
-            )
+            parts = [nc.vector, nc.gpsimd] if u == len(UNITS) - 1 else [nc.gpsimd]
+            count = HEADS // len(parts)
+            for k, engine in enumerate(parts):
+                heads = slice(k * count, (k + 1) * count)
+                engine.tensor_tensor(
+                    out=block_of(b, i, j)[:, heads, :],
+                    in0=by_head[u][:, heads, :],
+                    in1=share[u][:].unsqueeze(1).to_broadcast([P, count, P]),
+                    op=ALU.mult,
+                )
 
         def mirror(u):
             b, i, j = UNITS[u]
@@ -213,43 +258,40 @@ def tile_channelgroupattention_pa_t_kernel(tc, qkv_bn, gra_sharp, out_0, out_1):
                 nc.sync.dma_start(
                     out=attn_rows[:, t, :, J * width : (J + 1) * width], in_=panel[b][J][:, t, :, :]
                 )
-            column_fill[b][j] += 1
-            if column_fill[b][j] == CT:
-                return [(b, j, part) for part in range(HEADS // PIECE_HEADS)]
-            return []
 
-        def regroup(piece):
-            b, j, part = piece
+        def mirror_and_store(u):
+            b, i, j = UNITS[u]
+            if i != j:
+                mirror(u)
+                block_written(b, j, i)
+            block_written(b, i, j)
+
+        def regroup(b, j, n0, engine):
             first = (j % PANEL_TILES) * P
-            heads = slice(part * PIECE_HEADS, (part + 1) * PIECE_HEADS)
-            by_word = panel[b][j // PANEL_TILES][:, :, heads, first : first + P].rearrange(
-                "p t n c -> p n c t"
-            )
+            by_word = panel[b][j // PANEL_TILES][:, :, n0 : n0 + PIECE_HEADS, first : first + P]
             a_grouped = a_mx.tile([P, PIECE_HEADS, P, CT], BF16, align_bytes=64)
-            if part == 0:
-                nc.scalar.copy(out=a_grouped[:], in_=by_word)
-            else:
-                nc.vector.tensor_copy(out=a_grouped[:], in_=by_word)
-            return piece, a_grouped
+            copy_words(engine, a_grouped[:], by_word.rearrange("p t n c -> p n c t"))
+            pieces[b, j, n0] = a_grouped
 
-        def quantise(piece, a_grouped):
+        def quantise(b, j, n0):
             a_codes = a_mx.tile([P, PIECE_HEADS * P], U32, align_bytes=64)
             a_scales = a_mx.tile([P, PIECE_HEADS * P], U8, align_bytes=64)
             nc.vector.quantize_mx(
                 out=a_codes[:].bitcast(FP8X4),
                 scales=a_scales[:],
-                in_=a_grouped[:].rearrange("p n c t -> p (n c t)"),
+                in_=pieces[b, j, n0][:].rearrange("p n c t -> p (n c t)"),
             )
-            return piece, a_codes, a_scales
+            pieces[b, j, n0] = a_codes, a_scales
 
-        def multiply(piece, a_codes, a_scales):
-            b, j, part = piece
+        def multiply_and_store(b, j, n0, engines, tag, tag_bufs):
+            a_codes, a_scales = pieces[b, j, n0]
+            tiles = PIECE_HEADS * KT
             accs = []
-            for half in range(PIECE_HEADS * KT // 4):
-                acc = psum.tile([P, 4, P], F32, tag="flip", bufs=3)
+            for half in range(tiles // 4):
+                acc = psum.tile([P, 4, P], F32, name="acc", tag=tag, bufs=tag_bufs)
                 for k in range(4):
                     n = (half * 4 + k) // KT
-                    m = part * PIECE_HEADS * KT + half * 4 + k
+                    m = n0 * KT + half * 4 + k
                     nc.tensor.matmul_mx(
                         out=acc[:, k, :],
                         lhsT=q_codes[b][:, m * P : (m + 1) * P].bitcast(FP8X4),
@@ -260,55 +302,51 @@ def tile_channelgroupattention_pa_t_kernel(tc, qkv_bn, gra_sharp, out_0, out_1):
                         stop=True,
                     )
                 accs.append(acc)
-            return piece, accs
-
-        def store_h(piece, accs):
-            b, j, part = piece
-            tiles = PIECE_HEADS * KT
             h_sb = h_pool.tile([P, tiles, P], F32)
             for half in range(tiles // 4):
-                nc.scalar.copy(out=h_sb[:, half * 4 : (half + 1) * 4, :], in_=accs[half][:])
+                target = h_sb[:, half * 4 : (half + 1) * 4, :]
+                if engines[half] == "scalar":
+                    nc.scalar.copy(out=target, in_=accs[half][:])
+                else:
+                    nc.vector.tensor_copy(out=target, in_=accs[half][:])
             h_rows = out_0[b].rearrange("(m w) c -> w m c", w=P)
             nc.sync.dma_start(
-                out=h_rows[:, part * tiles : (part + 1) * tiles, j * P : (j + 1) * P], in_=h_sb[:]
+                out=h_rows[:, n0 * KT : n0 * KT + tiles, j * P : (j + 1) * P], in_=h_sb[:]
             )
-
-        def is_unit(u):
-            return 0 <= u < len(UNITS)
 
         for b in range(BATCH):
             load_q(b)
-        waiting, regrouped, quantised, multiplied = [], [], [], []
-        for step in range(FIRST_STEP, LAST_STEP):
-            if is_unit(step - LAG_EXP):
-                exponential(step - LAG_EXP)
-            if is_unit(step + AHEAD_SCORES):
-                scores(step + AHEAD_SCORES)
-            if is_unit(step - LAG_SUM):
-                sum_heads(step - LAG_SUM)
-            for item in multiplied:
-                store_h(*item)
-            if is_unit(step - LAG_MIRROR):
-                b, i, j = UNITS[step - LAG_MIRROR]
-                if i != j:
-                    mirror(step - LAG_MIRROR)
-                    waiting.extend(block_written(b, j, i))
-                waiting.extend(block_written(b, i, j))
-            multiplied = [multiply(*item) for item in quantised]
-            to_quantise = regrouped
-            if 0 <= step < BATCH * Q_PIECES:
-                regroup_q(step // Q_PIECES, step % Q_PIECES)
-            if is_unit(step):
-                subtract_maximum(step)
-            regrouped = [regroup(piece) for piece in waiting[:PIECES_PER_STEP]]
-            waiting = waiting[PIECES_PER_STEP:]
-            quantised = [quantise(*item) for item in to_quantise]
-            if 0 <= step - 1 < BATCH * Q_PIECES:
-                quantise_q((step - 1) // Q_PIECES, (step - 1) % Q_PIECES)
-            if is_unit(step - LAG_SUM):
-                reciprocal(step - LAG_SUM)
-            if is_unit(step - LAG_NORMALISE):
-                normalise(step - LAG_NORMALISE)
-            if step - FIRST_STEP < BATCH * CT:
-                turn_q((step - FIRST_STEP) // CT, (step - FIRST_STEP) % CT)
-        assert not (waiting or regrouped or quantised or multiplied)
+
+        writings = []
+
+        def write_at(time, action, *args):
+            writings.append((time, len(writings), action, args))
+
+        for u in range(len(UNITS)):
+            write_at(u + SCORES, scores, u)
+            write_at(u, subtract_maximum, u)
+            write_at(u + EXPONENTIAL, exponential, u)
+            write_at(u + (SUM_TENSOR if summed_on_tensor(u) else SUM_VECTOR), sum_heads, u)
+            write_at(u + RECIPROCAL, reciprocal, u)
+            write_at(u + NORMALISE, normalise, u)
+            write_at(u + MIRROR, mirror_and_store, u)
+        for b in range(BATCH):
+            for t in range(CT):
+                write_at(TURN_FIRST[b] + t, turn_q, b, t)
+            for piece in range(Q_PIECES):
+                write_at(Q_REGROUP_FIRST[b] + piece, regroup_q, b, piece)
+                write_at(Q_REGROUP_FIRST[b] + piece + Q_QUANTISE, quantise_q, b, piece)
+            for j in range(CT):
+                last = max(u for u in range(len(UNITS)) if UNITS[u][0] == b and j in UNITS[u][1:])
+                ending = last >= len(UNITS) - 2
+                for k in range(HEADS // PIECE_HEADS):
+                    piece = (b, j, k * PIECE_HEADS)
+                    time = last + (REGROUP_LAST if j == CT - 1 else REGROUP) + k * NEXT_PIECE
+                    engine = ("vector" if k == 0 else "scalar") if ending else "scalar"
+                    write_at(time, regroup, *piece, engine)
+                    write_at(time + QUANTISE, quantise, *piece)
+                    engines = ("scalar", "vector") if ending else ("scalar", "scalar")
+                    tag, tag_bufs = ("scores", 4) if ending else ("flip", 3)
+                    write_at(time + MULTIPLY, multiply_and_store, *piece, engines, tag, tag_bufs)
+        for time, index, action, args in sorted(writings, key=lambda writing: writing[:2]):
+            action(*args)

@@ -54,14 +54,13 @@ def tile_channelgroupattention_pa_t_kernel(tc, qkv_bn, gra_sharp, out_0, out_1):
     nc = tc.nc
     with ExitStack() as stack:
         const = stack.enter_context(tc.tile_pool(name="const", bufs=1))
-        natural = stack.enter_context(tc.tile_pool(name="natural", bufs=2))
+        large = stack.enter_context(tc.tile_pool(name="large", bufs=3))
         turned = stack.enter_context(tc.tile_pool(name="turned", bufs=2))
         q_mx = stack.enter_context(tc.tile_pool(name="q_mx", bufs=2))
         stage = stack.enter_context(tc.tile_pool(name="stage", bufs=2))
         panels = stack.enter_context(tc.tile_pool(name="panels", bufs=3))
         work = stack.enter_context(tc.tile_pool(name="work", bufs=2))
         a_mx = stack.enter_context(tc.tile_pool(name="a_mx", bufs=2))
-        h_pool = stack.enter_context(tc.tile_pool(name="h_pool", bufs=4))
         psum = stack.enter_context(tc.psum_pool(name="psum", bufs=2))
         stack.enter_context(tc.manual_schedule())
 
@@ -83,7 +82,7 @@ def tile_channelgroupattention_pa_t_kernel(tc, qkv_bn, gra_sharp, out_0, out_1):
 
         q_nat, q_t, q_grouped, q_codes, q_scales, panel = {}, {}, {}, {}, {}, {}
         banks, e, by_head, total, share = {}, {}, {}, {}, {}
-        row_fill, pieces = {}, {}
+        row_fill, pieces, h_sb, h_fill = {}, {}, {}, {}
 
         def gpsimd_copy(out, in_):
             nc.gpsimd.tensor_scalar(
@@ -105,7 +104,7 @@ def tile_channelgroupattention_pa_t_kernel(tc, qkv_bn, gra_sharp, out_0, out_1):
                 gpsimd_copy(out, in_)
 
         def load_q(b):
-            q_nat[b] = natural.tile([P, CT, TOKENS], BF16, name="q_nat")
+            q_nat[b] = large.tile([P, CT, TOKENS], BF16, name="q_nat", tag="large")
             for t in range(CT):
                 nc.sync.dma_start(out=q_nat[b][:, t, :], in_=qkv_bn[b, t * P : (t + 1) * P, :])
             q_t[b] = turned.tile([P, TOKEN_TILES, CHANNELS], BF16, name="q_t")
@@ -302,17 +301,26 @@ def tile_channelgroupattention_pa_t_kernel(tc, qkv_bn, gra_sharp, out_0, out_1):
                         stop=True,
                     )
                 accs.append(acc)
-            h_sb = h_pool.tile([P, tiles, P], F32)
+            J, first = j // PANEL_TILES, (j % PANEL_TILES) * P
+            if (b, J) not in h_sb:
+                h_sb[b, J] = large.tile(
+                    [P, TOKEN_TILES, PANEL_TILES * P], F32, name="h_sb", tag="large"
+                )
             for half in range(tiles // 4):
-                target = h_sb[:, half * 4 : (half + 1) * 4, :]
+                m = n0 * KT + half * 4
+                target = h_sb[b, J][:, m : m + 4, first : first + P]
                 if engines[half] == "scalar":
                     nc.scalar.copy(out=target, in_=accs[half][:])
                 else:
                     nc.vector.tensor_copy(out=target, in_=accs[half][:])
-            h_rows = out_0[b].rearrange("(m w) c -> w m c", w=P)
-            nc.sync.dma_start(
-                out=h_rows[:, n0 * KT : n0 * KT + tiles, j * P : (j + 1) * P], in_=h_sb[:]
-            )
+            h_fill[b, J, n0] = h_fill.get((b, J, n0), 0) + 1
+            if h_fill[b, J, n0] == PANEL_TILES:
+                h_rows = out_0[b].rearrange("(m w) c -> w m c", w=P)
+                rows = slice(n0 * KT, n0 * KT + tiles)
+                width = PANEL_TILES * P
+                nc.sync.dma_start(
+                    out=h_rows[:, rows, J * width : (J + 1) * width], in_=h_sb[b, J][:, rows, :]
+                )
 
         for b in range(BATCH):
             load_q(b)

@@ -24,28 +24,31 @@ BANK_COLUMNS = P // BANKS
 PANEL_TILES = 2
 PANELS = CT // PANEL_TILES
 PIECE_HEADS = 4
-Q_PIECES = 4
+Q_PIECES = 16
 Q_PIECE_TOKENS = TOKENS // Q_PIECES
 
 UNITS = [(b, i, j) for b in range(BATCH) for i in range(CT) for j in range(i, CT)]
 BATCH_UNITS = len(UNITS) // BATCH
 
-SCORES = -0.9
-EXPONENTIAL = 0.4
-SUM_TENSOR = 1.0
-SUM_VECTOR = 1.4
-RECIPROCAL = 1.7
-NORMALISE = 1.7
-MIRROR = 2.6
-REGROUP = 3.0
-REGROUP_LAST = 3.2
-NEXT_PIECE = 0.9
-QUANTISE = 1.1
-MULTIPLY = 1.8
+SCORES = -0.25
+EXPONENTIAL = 0.5
+ADD_HALVES = 1.25
+SUM_HEADS = 2.25
+RECIPROCAL = 2.75
+NORMALISE = 3.0
+MIRROR = 3.75
+REGROUP = 4.5
+REGROUP_LAST = 5.5
+NEXT_PIECE = 1.0
+QUANTISE = 1.0
+MULTIPLY = 2.5
 E_BUFFERS = 4
-TURN_FIRST = (-1.0, 2.0)
-Q_REGROUP_FIRST = (0.0, 6.0)
-Q_QUANTISE = 1.75
+TURN_FIRST = (-1.0, 4.0)
+Q_REGROUP_FIRST = (0.0, 1.5)
+Q_REGROUP_STEP = (0.3, 1.0)
+Q_QUANTISE = (0.5, 0.75)
+LAST_REGROUP = {(2, 0): "vector", (2, 1): "scalar", (3, 0): "scalar", (3, 1): "gpsimd"}
+LAST_UNITS = 3
 
 FLOPS = 2 * 2 * BATCH * HEADS * CHANNELS * CHANNELS * HEAD_TOKENS
 
@@ -81,7 +84,7 @@ def tile_channelgroupattention_pa_t_kernel(tc, qkv_bn, gra_sharp, out_0, out_1):
         nc.scalar.activation(out=warm[:], in_=warm[:], func=ACT.Exp)
 
         q_nat, q_t, q_grouped, q_codes, q_scales, panel = {}, {}, {}, {}, {}, {}
-        banks, e, by_head, total, share = {}, {}, {}, {}, {}
+        banks, e, halves, total, share = {}, {}, {}, {}, {}
         row_fill, pieces, h_sb, h_fill = {}, {}, {}, {}
 
         def gpsimd_copy(out, in_):
@@ -90,18 +93,16 @@ def tile_channelgroupattention_pa_t_kernel(tc, qkv_bn, gra_sharp, out_0, out_1):
             )
 
         def copy_words(engine, words, by_word):
-            if len(words.shape) == 3:
-                out = words.rearrange("p (c i) t -> p c t i", i=4)
-                in_ = by_word.rearrange("p (c i) t -> p c t i", i=4)
-            else:
-                out = words.rearrange("p n (c i) t -> p n c t i", i=4)
-                in_ = by_word.rearrange("p n (c i) t -> p n c t i", i=4)
+            if engine == "gpsimd":
+                gpsimd_copy(words, by_word)
+                return
+            axes = "p n" if len(words.shape) == 4 else "p"
+            out = words.rearrange(axes + " (c i) t -> " + axes + " c t i", i=4)
+            in_ = by_word.rearrange(axes + " (c i) t -> " + axes + " c t i", i=4)
             if engine == "scalar":
                 nc.scalar.copy(out=out, in_=in_)
-            elif engine == "vector":
-                nc.vector.tensor_copy(out=out, in_=in_)
             else:
-                gpsimd_copy(out, in_)
+                nc.vector.tensor_copy(out=out, in_=in_)
 
         def load_q(b):
             q_nat[b] = large.tile([P, CT, TOKENS], BF16, name="q_nat", tag="large")
@@ -125,10 +126,10 @@ def tile_channelgroupattention_pa_t_kernel(tc, qkv_bn, gra_sharp, out_0, out_1):
         def regroup_q(b, piece):
             cols = slice(piece * Q_PIECE_TOKENS, (piece + 1) * Q_PIECE_TOKENS)
             q_grouped[b, piece] = stage.tile(
-                [P, Q_PIECE_TOKENS, CT], BF16, name="q_grouped", align_bytes=64
+                [P, Q_PIECE_TOKENS, CT], BF16, name="q_grouped%d" % b, bufs=2 - b, align_bytes=64
             )
             by_word = q_nat[b][:, :, cols].rearrange("p t w -> p w t")
-            copy_words("gpsimd", q_grouped[b, piece][:], by_word)
+            copy_words("scalar" if b == 0 else "gpsimd", q_grouped[b, piece][:], by_word)
 
         def quantise_q(b, piece):
             cols = slice(piece * Q_PIECE_TOKENS, (piece + 1) * Q_PIECE_TOKENS)
@@ -159,9 +160,6 @@ def tile_channelgroupattention_pa_t_kernel(tc, qkv_bn, gra_sharp, out_0, out_1):
                         )
                 banks[u].append(bank)
 
-        def summed_on_tensor(u):
-            return u % 3 != 1
-
         def subtract_maximum(u):
             top = work.tile([P, BANKS, BANK_COLUMNS], F32)
             for half in range(BANKS):
@@ -171,46 +169,38 @@ def tile_channelgroupattention_pa_t_kernel(tc, qkv_bn, gra_sharp, out_0, out_1):
                     axis=AXIS.X,
                     op=ALU.max,
                 )
-            if summed_on_tensor(u):
-                e[u] = work.tile([P, HEADS, P], F32, name="e", tag="e", bufs=E_BUFFERS)
-                by_head[u] = e[u][:]
-            else:
-                e[u] = work.tile([P, P, HEADS], F32, name="e", tag="e", bufs=E_BUFFERS)
-                by_head[u] = e[u][:].rearrange("p d n -> p n d")
+            e[u] = work.tile([P, HEADS, P], F32, name="e", bufs=E_BUFFERS)
             for half in range(BANKS):
                 columns = slice(half * BANK_COLUMNS, (half + 1) * BANK_COLUMNS)
-                if summed_on_tensor(u):
-                    nc.vector.tensor_tensor(
-                        out=e[u][:, :, columns],
-                        in0=banks[u][half][:],
-                        in1=top[:, half, :].unsqueeze(1).to_broadcast([P, HEADS, BANK_COLUMNS]),
-                        op=ALU.subtract,
-                    )
-                else:
-                    nc.vector.tensor_tensor(
-                        out=e[u][:, columns, :],
-                        in0=banks[u][half][:].rearrange("p n d -> p d n"),
-                        in1=top[:, half, :].unsqueeze(2).to_broadcast([P, BANK_COLUMNS, HEADS]),
-                        op=ALU.subtract,
-                    )
+                nc.vector.tensor_tensor(
+                    out=e[u][:, :, columns],
+                    in0=banks[u][half][:],
+                    in1=top[:, half, :].unsqueeze(1).to_broadcast([P, HEADS, BANK_COLUMNS]),
+                    op=ALU.subtract,
+                )
 
         def exponential(u):
             nc.scalar.activation(out=e[u][:], in_=e[u][:], func=ACT.Exp, scale=inv_sharp[:, 0:1])
 
+        def add_halves(u):
+            halves[u] = work.tile([P, HEADS // 2, P], F32, name="halves")
+            nc.vector.tensor_tensor(
+                out=halves[u][:],
+                in0=e[u][:, : HEADS // 2, :],
+                in1=e[u][:, HEADS // 2 :, :],
+                op=ALU.add,
+            )
+
         def sum_heads(u):
-            if summed_on_tensor(u):
-                total[u] = psum.tile([P, P], F32, name="total_t", tag="total", bufs=1)
-                for n in range(HEADS):
-                    nc.tensor.matmul(
-                        total[u][:],
-                        lhsT=ident_f32[:],
-                        rhs=e[u][:, n, :],
-                        start=(n == 0),
-                        stop=(n == HEADS - 1),
-                    )
-            else:
-                total[u] = work.tile([P, P], F32, name="total_v")
-                nc.vector.tensor_reduce(out=total[u][:], in_=e[u][:], axis=AXIS.X, op=ALU.add)
+            total[u] = psum.tile([P, P], F32, name="total", bufs=1)
+            for n in range(HEADS // 2):
+                nc.tensor.matmul(
+                    total[u][:],
+                    lhsT=ident_f32[:],
+                    rhs=halves[u][:, n, :],
+                    start=(n == 0),
+                    stop=(n == HEADS // 2 - 1),
+                )
 
         def reciprocal(u):
             share[u] = work.tile([P, P], F32, name="share", bufs=3)
@@ -224,16 +214,13 @@ def tile_channelgroupattention_pa_t_kernel(tc, qkv_bn, gra_sharp, out_0, out_1):
                     for J in range(PANELS)
                 ]
                 row_fill[b] = [[0] * CT for J in range(PANELS)]
-            parts = [nc.vector, nc.gpsimd] if u == len(UNITS) - 1 else [nc.gpsimd]
-            count = HEADS // len(parts)
-            for k, engine in enumerate(parts):
-                heads = slice(k * count, (k + 1) * count)
-                engine.tensor_tensor(
-                    out=block_of(b, i, j)[:, heads, :],
-                    in0=by_head[u][:, heads, :],
-                    in1=share[u][:].unsqueeze(1).to_broadcast([P, count, P]),
-                    op=ALU.mult,
-                )
+            engine = nc.vector if u >= len(UNITS) - LAST_UNITS else nc.gpsimd
+            engine.tensor_tensor(
+                out=block_of(b, i, j),
+                in0=e[u][:],
+                in1=share[u][:].unsqueeze(1).to_broadcast([P, HEADS, P]),
+                op=ALU.mult,
+            )
 
         def mirror(u):
             b, i, j = UNITS[u]
@@ -334,7 +321,8 @@ def tile_channelgroupattention_pa_t_kernel(tc, qkv_bn, gra_sharp, out_0, out_1):
             write_at(u + SCORES, scores, u)
             write_at(u, subtract_maximum, u)
             write_at(u + EXPONENTIAL, exponential, u)
-            write_at(u + (SUM_TENSOR if summed_on_tensor(u) else SUM_VECTOR), sum_heads, u)
+            write_at(u + ADD_HALVES, add_halves, u)
+            write_at(u + SUM_HEADS, sum_heads, u)
             write_at(u + RECIPROCAL, reciprocal, u)
             write_at(u + NORMALISE, normalise, u)
             write_at(u + MIRROR, mirror_and_store, u)
@@ -342,18 +330,19 @@ def tile_channelgroupattention_pa_t_kernel(tc, qkv_bn, gra_sharp, out_0, out_1):
             for t in range(CT):
                 write_at(TURN_FIRST[b] + t, turn_q, b, t)
             for piece in range(Q_PIECES):
-                write_at(Q_REGROUP_FIRST[b] + piece, regroup_q, b, piece)
-                write_at(Q_REGROUP_FIRST[b] + piece + Q_QUANTISE, quantise_q, b, piece)
+                time = Q_REGROUP_FIRST[b] + piece * Q_REGROUP_STEP[b]
+                write_at(time, regroup_q, b, piece)
+                write_at(time + Q_QUANTISE[b], quantise_q, b, piece)
             for j in range(CT):
                 last = max(u for u in range(len(UNITS)) if UNITS[u][0] == b and j in UNITS[u][1:])
                 ending = last >= len(UNITS) - 2
                 for k in range(HEADS // PIECE_HEADS):
                     piece = (b, j, k * PIECE_HEADS)
                     time = last + (REGROUP_LAST if j == CT - 1 else REGROUP) + k * NEXT_PIECE
-                    engine = ("vector" if k == 0 else "scalar") if ending else "scalar"
+                    engine = LAST_REGROUP[j, k] if ending else "scalar"
                     write_at(time, regroup, *piece, engine)
                     write_at(time + QUANTISE, quantise, *piece)
-                    engines = ("scalar", "vector") if ending else ("scalar", "scalar")
+                    engines = ("vector", "scalar") if b else ("scalar", "vector")
                     tag, tag_bufs = ("scores", 4) if ending else ("flip", 3)
                     write_at(time + MULTIPLY, multiply_and_store, *piece, engines, tag, tag_bufs)
         for time, index, action, args in sorted(writings, key=lambda writing: writing[:2]):

@@ -44,10 +44,10 @@ QUANTISE = 1.0
 MULTIPLY = 2.5
 E_BUFFERS = 4
 TURN_FIRST = (-1.0, 4.0)
-Q_REGROUP_FIRST = (0.0, 1.5)
-Q_REGROUP_STEP = (0.3, 1.0)
+Q_REGROUP_FIRST = (0.75, 1.5)
+Q_REGROUP_STEP = (0.5, 1.0)
 Q_QUANTISE = (0.5, 0.75)
-LAST_REGROUP = {(2, 0): "vector", (2, 1): "scalar", (3, 0): "scalar", (3, 1): "gpsimd"}
+LAST_REGROUP = {(2, 0): "vector", (2, 1): "scalar", (3, 0): "vector", (3, 1): "scalar"}
 LAST_UNITS = 3
 
 FLOPS = 2 * 2 * BATCH * HEADS * CHANNELS * CHANNELS * HEAD_TOKENS
@@ -97,8 +97,8 @@ def tile_channelgroupattention_pa_t_kernel(tc, qkv_bn, gra_sharp, out_0, out_1):
                 gpsimd_copy(words, by_word)
                 return
             axes = "p n" if len(words.shape) == 4 else "p"
-            out = words.rearrange(axes + " (c i) t -> " + axes + " c t i", i=4)
-            in_ = by_word.rearrange(axes + " (c i) t -> " + axes + " c t i", i=4)
+            out = words.rearrange(axes + " (c i) t -> " + axes + " c t i", i=2)
+            in_ = by_word.rearrange(axes + " (c i) t -> " + axes + " c t i", i=2)
             if engine == "scalar":
                 nc.scalar.copy(out=out, in_=in_)
             else:

@@ -43,6 +43,8 @@ NEXT_PIECE = 1.0
 QUANTISE = 1.0
 MULTIPLY = 2.5
 E_BUFFERS = 4
+WARM_COLUMNS = 512
+WARM_MATMULS = 5
 TURN_FIRST = (-1.0, 4.0)
 Q_REGROUP_FIRST = (0.75, 1.5)
 Q_REGROUP_STEP = (0.5, 1.0)
@@ -73,11 +75,18 @@ def tile_channelgroupattention_pa_t_kernel(tc, qkv_bn, gra_sharp, out_0, out_1):
         make_identity(nc, ident_f32[:])
 
         sharp_bf = const.tile([P, 1], BF16)
-        nc.sync.dma_start(out=sharp_bf[:], in_=gra_sharp.partition_broadcast(P))
         sharp = const.tile([P, 1], F32)
-        nc.vector.tensor_copy(out=sharp[:], in_=sharp_bf[:])
         inv_sharp = const.tile([P, 1], F32)
-        nc.vector.reciprocal(out=inv_sharp[:], in_=sharp[:])
+
+        def invert_sharp():
+            nc.vector.tensor_copy(out=sharp[:], in_=sharp_bf[:])
+            nc.vector.reciprocal(out=inv_sharp[:], in_=sharp[:])
+
+        zeros = const.tile([P, WARM_COLUMNS], BF16)
+        nc.vector.memset(zeros[:], 0.0)
+        for k in range(WARM_MATMULS):
+            unused = psum.tile([P, WARM_COLUMNS], F32, name="unused", tag="scores", bufs=4)
+            nc.tensor.matmul(unused[:], lhsT=zeros[:, :P], rhs=zeros[:], start=True, stop=True)
 
         warm = const.tile([P, 1], F32)
         nc.vector.memset(warm[:], 0.0)
@@ -97,8 +106,8 @@ def tile_channelgroupattention_pa_t_kernel(tc, qkv_bn, gra_sharp, out_0, out_1):
                 gpsimd_copy(words, by_word)
                 return
             axes = "p n" if len(words.shape) == 4 else "p"
-            out = words.rearrange(axes + " (c i) t -> " + axes + " c t i", i=2)
-            in_ = by_word.rearrange(axes + " (c i) t -> " + axes + " c t i", i=2)
+            out = words.rearrange(axes + " (c i) t -> " + axes + " c t i", i=4)
+            in_ = by_word.rearrange(axes + " (c i) t -> " + axes + " c t i", i=4)
             if engine == "scalar":
                 nc.scalar.copy(out=out, in_=in_)
             else:
@@ -107,7 +116,14 @@ def tile_channelgroupattention_pa_t_kernel(tc, qkv_bn, gra_sharp, out_0, out_1):
         def load_q(b):
             q_nat[b] = large.tile([P, CT, TOKENS], BF16, name="q_nat", tag="large")
             for t in range(CT):
-                nc.sync.dma_start(out=q_nat[b][:, t, :], in_=qkv_bn[b, t * P : (t + 1) * P, :])
+                parts = 2 if (b, t) == (0, 0) else 1
+                for part in range(parts):
+                    cols = slice(part * TOKENS // parts, (part + 1) * TOKENS // parts)
+                    nc.sync.dma_start(
+                        out=q_nat[b][:, t, cols], in_=qkv_bn[b, t * P : (t + 1) * P, cols]
+                    )
+                if (b, t) == (0, 1):
+                    nc.sync.dma_start(out=sharp_bf[:], in_=gra_sharp.partition_broadcast(P))
             q_t[b] = turned.tile([P, TOKEN_TILES, CHANNELS], BF16, name="q_t")
             q_codes[b] = q_mx.tile([P, TOKENS], U32, name="q_codes", align_bytes=64)
             q_scales[b] = q_mx.tile([P, TOKENS], U8, name="q_scales", align_bytes=64)
@@ -317,6 +333,7 @@ def tile_channelgroupattention_pa_t_kernel(tc, qkv_bn, gra_sharp, out_0, out_1):
         def write_at(time, action, *args):
             writings.append((time, len(writings), action, args))
 
+        write_at(0.25, invert_sharp)
         for u in range(len(UNITS)):
             write_at(u + SCORES, scores, u)
             write_at(u, subtract_maximum, u)

@@ -106,8 +106,8 @@ def tile_channelgroupattention_pa_t_kernel(tc, qkv_bn, gra_sharp, out_0, out_1):
                 gpsimd_copy(words, by_word)
                 return
             axes = "p n" if len(words.shape) == 4 else "p"
-            out = words.rearrange(axes + " (c i) t -> " + axes + " c t i", i=4)
-            in_ = by_word.rearrange(axes + " (c i) t -> " + axes + " c t i", i=4)
+            out = words.rearrange(axes + " (c i) t -> " + axes + " c t i", i=8)
+            in_ = by_word.rearrange(axes + " (c i) t -> " + axes + " c t i", i=8)
             if engine == "scalar":
                 nc.scalar.copy(out=out, in_=in_)
             else:

from contextlib import ExitStack

import concourse.mybir as mybir
from concourse.masks import make_identity

F32 = mybir.dt.float32
BF16 = mybir.dt.bfloat16
U32 = mybir.dt.uint32
U8 = mybir.dt.uint8
FP8X4 = mybir.dt.float8_e4m3fn_x4
ALU = mybir.AluOpType
ACT = mybir.ActivationFunctionType
AXIS = mybir.AxisListType

P = 128
BATCH, CHANNELS, TOKENS, HEADS = 2, 512, 2048, 8
HEAD_TOKENS = TOKENS // HEADS
CT = CHANNELS // P
KT = HEAD_TOKENS // P
TOKEN_TILES = TOKENS // P
BANK_HEADS = 4
BANKS = HEADS // BANK_HEADS
BANK_COLUMNS = P // BANKS
PANEL_TILES = 2
PANELS = CT // PANEL_TILES
PIECE_HEADS = 4
Q_PIECES = 16
Q_PIECE_TOKENS = TOKENS // Q_PIECES

UNITS = [(b, i, j) for b in range(BATCH) for i in range(CT) for j in range(i, CT)]
BATCH_UNITS = len(UNITS) // BATCH

SCORES = -0.25
EXPONENTIAL = 0.5
ADD_HALVES = 1.25
SUM_HEADS = 2.25
RECIPROCAL = 2.75
NORMALISE = 3.0
MIRROR = 3.75
REGROUP = 4.5
REGROUP_LAST = 5.5
NEXT_PIECE = 1.0
QUANTISE = 1.0
MULTIPLY = 2.5
E_BUFFERS = 4
WARM_COLUMNS = 512
WARM_MATMULS = 5
TURN_FIRST = (-1.0, 4.0)
Q_REGROUP_FIRST = (0.75, 1.5)
Q_REGROUP_STEP = (0.5, 1.0)
Q_QUANTISE = (0.5, 0.75)
LAST_REGROUP = {(2, 0): "vector", (2, 1): "scalar", (3, 0): "vector", (3, 1): "scalar"}
LAST_UNITS = 3

FLOPS = 2 * 2 * BATCH * HEADS * CHANNELS * CHANNELS * HEAD_TOKENS


def tile_channelgroupattention_pa_t_kernel(tc, qkv_bn, gra_sharp, out_0, out_1):
    nc = tc.nc
    with ExitStack() as stack:
        const = stack.enter_context(tc.tile_pool(name="const", bufs=1))
        large = stack.enter_context(tc.tile_pool(name="large", bufs=3))
        turned = stack.enter_context(tc.tile_pool(name="turned", bufs=2))
        q_mx = stack.enter_context(tc.tile_pool(name="q_mx", bufs=2))
        stage = stack.enter_context(tc.tile_pool(name="stage", bufs=2))
        panels = stack.enter_context(tc.tile_pool(name="panels", bufs=3))
        work = stack.enter_context(tc.tile_pool(name="work", bufs=2))
        a_mx = stack.enter_context(tc.tile_pool(name="a_mx", bufs=2))
        psum = stack.enter_context(tc.psum_pool(name="psum", bufs=2))
        stack.enter_context(tc.manual_schedule())

        ident_bf = const.tile([P, P], BF16)
        make_identity(nc, ident_bf[:])
        ident_f32 = const.tile([P, P], F32)
        make_identity(nc, ident_f32[:])

        sharp_bf = const.tile([P, 1], BF16)
        sharp = const.tile([P, 1], F32)
        inv_sharp = const.tile([P, 1], F32)

        def invert_sharp():
            nc.vector.tensor_copy(out=sharp[:], in_=sharp_bf[:])
            nc.vector.reciprocal(out=inv_sharp[:], in_=sharp[:])

        zeros = const.tile([P, WARM_COLUMNS], BF16)
        nc.vector.memset(zeros[:], 0.0)
        for k in range(WARM_MATMULS):
            unused = psum.tile([P, WARM_COLUMNS], F32, name="unused", tag="scores", bufs=4)
            nc.tensor.matmul(unused[:], lhsT=zeros[:, :P], rhs=zeros[:], start=True, stop=True)

        warm = const.tile([P, 1], F32)
        nc.vector.memset(warm[:], 0.0)
        nc.scalar.activation(out=warm[:], in_=warm[:], func=ACT.Exp)

        q_nat, q_t, q_grouped, q_codes, q_scales, panel = {}, {}, {}, {}, {}, {}
        banks, e, halves, total, share = {}, {}, {}, {}, {}
        row_fill, pieces, h_sb, h_fill = {}, {}, {}, {}

        def gpsimd_copy(out, in_):
            nc.gpsimd.tensor_scalar(
                out=out, in0=in_, scalar1=1.0, scalar2=0.0, op0=ALU.mult, op1=ALU.add
            )

        def copy_words(engine, words, by_word):
            if engine == "gpsimd":
                gpsimd_copy(words, by_word)
                return
            axes = "p n" if len(words.shape) == 4 else "p"
            out = words.rearrange(axes + " (c i) t -> " + axes + " c t i", i=8)
            in_ = by_word.rearrange(axes + " (c i) t -> " + axes + " c t i", i=8)
            if engine == "scalar":
                nc.scalar.copy(out=out, in_=in_)
            else:
                nc.vector.tensor_copy(out=out, in_=in_)

        def load_q(b):
            q_nat[b] = large.tile([P, CT, TOKENS], BF16, name="q_nat", tag="large")
            for t in range(CT):
                parts = 2 if (b, t) == (0, 0) else 1
                for part in range(parts):
                    cols = slice(part * TOKENS // parts, (part + 1) * TOKENS // parts)
                    nc.sync.dma_start(
                        out=q_nat[b][:, t, cols], in_=qkv_bn[b, t * P : (t + 1) * P, cols]
                    )
                if (b, t) == (0, 1):
                    nc.sync.dma_start(out=sharp_bf[:], in_=gra_sharp.partition_broadcast(P))
            q_t[b] = turned.tile([P, TOKEN_TILES, CHANNELS], BF16, name="q_t")
            q_codes[b] = q_mx.tile([P, TOKENS], U32, name="q_codes", align_bytes=64)
            q_scales[b] = q_mx.tile([P, TOKENS], U8, name="q_scales", align_bytes=64)

        def turn_q(b, t):
            for g in range(TOKEN_TILES // 4):
                flipped = psum.tile([P, 4, P], BF16, tag="flip", bufs=3)
                for k in range(4):
                    m = 4 * g + k
                    nc.tensor.transpose(
                        flipped[:, k, :], q_nat[b][:, t, m * P : (m + 1) * P], ident_bf[:]
                    )
                target = q_t[b][:, 4 * g : 4 * g + 4, t * P : (t + 1) * P]
                nc.scalar.copy(out=target, in_=flipped[:])

        def regroup_q(b, piece):
            cols = slice(piece * Q_PIECE_TOKENS, (piece + 1) * Q_PIECE_TOKENS)
            q_grouped[b, piece] = stage.tile(
                [P, Q_PIECE_TOKENS, CT], BF16, name="q_grouped%d" % b, bufs=2 - b, align_bytes=64
            )
            by_word = q_nat[b][:, :, cols].rearrange("p t w -> p w t")
            copy_words("scalar" if b == 0 else "gpsimd", q_grouped[b, piece][:], by_word)

        def quantise_q(b, piece):
            cols = slice(piece * Q_PIECE_TOKENS, (piece + 1) * Q_PIECE_TOKENS)
            nc.vector.quantize_mx(
                out=q_codes[b][:, cols].bitcast(FP8X4),
                scales=q_scales[b][:, cols],
                in_=q_grouped[b, piece][:].rearrange("p w t -> p (w t)"),
            )

        def block_of(b, t, j):
            first = (j % PANEL_TILES) * P
            return panel[b][j // PANEL_TILES][:, t, :, first : first + P]

        def scores(u):
            b, i, j = UNITS[u]
            banks[u] = []
            for half in range(BANKS):
                first = j * P + half * BANK_COLUMNS
                bank = psum.tile([P, HEADS, BANK_COLUMNS], F32, tag="scores", bufs=4)
                for n in range(HEADS):
                    for kt in range(KT):
                        nc.tensor.matmul(
                            bank[:, n, :],
                            lhsT=q_t[b][:, n * KT + kt, i * P : (i + 1) * P],
                            rhs=q_t[b][:, n * KT + kt, first : first + BANK_COLUMNS],
                            start=(kt == 0),
                            stop=(kt == KT - 1),
                        )
                banks[u].append(bank)

        def subtract_maximum(u):
            top = work.tile([P, BANKS, BANK_COLUMNS], F32)
            for half in range(BANKS):
                nc.vector.tensor_reduce(
                    out=top[:, half, :],
                    in_=banks[u][half][:].rearrange("p n d -> p d n"),
                    axis=AXIS.X,
                    op=ALU.max,
                )
            e[u] = work.tile([P, HEADS, P], F32, name="e", bufs=E_BUFFERS)
            for half in range(BANKS):
                columns = slice(half * BANK_COLUMNS, (half + 1) * BANK_COLUMNS)
                nc.vector.tensor_tensor(
                    out=e[u][:, :, columns],
                    in0=banks[u][half][:],
                    in1=top[:, half, :].unsqueeze(1).to_broadcast([P, HEADS, BANK_COLUMNS]),
                    op=ALU.subtract,
                )

        def exponential(u):
            nc.scalar.activation(out=e[u][:], in_=e[u][:], func=ACT.Exp, scale=inv_sharp[:, 0:1])

        def add_halves(u):
            halves[u] = work.tile([P, HEADS // 2, P], F32, name="halves")
            nc.vector.tensor_tensor(
                out=halves[u][:],
                in0=e[u][:, : HEADS // 2, :],
                in1=e[u][:, HEADS // 2 :, :],
                op=ALU.add,
            )

        def sum_heads(u):
            total[u] = psum.tile([P, P], F32, name="total", bufs=1)
            for n in range(HEADS // 2):
                nc.tensor.matmul(
                    total[u][:],
                    lhsT=ident_f32[:],
                    rhs=halves[u][:, n, :],
                    start=(n == 0),
                    stop=(n == HEADS // 2 - 1),
                )

        def reciprocal(u):
            share[u] = work.tile([P, P], F32, name="share", bufs=3)
            nc.vector.reciprocal(out=share[u][:], in_=total[u][:])

        def normalise(u):
            b, i, j = UNITS[u]
            if u % BATCH_UNITS == 0:
                panel[b] = [
                    panels.tile([P, CT, HEADS, PANEL_TILES * P], F32, name="panel", tag="panel")
                    for J in range(PANELS)
                ]
                row_fill[b] = [[0] * CT for J in range(PANELS)]
            engine = nc.vector if u >= len(UNITS) - LAST_UNITS else nc.gpsimd
            engine.tensor_tensor(
                out=block_of(b, i, j),
                in0=e[u][:],
                in1=share[u][:].unsqueeze(1).to_broadcast([P, HEADS, P]),
                op=ALU.mult,
            )

        def mirror(u):
            b, i, j = UNITS[u]
            for half in range(BANKS):
                heads = slice(half * BANK_HEADS, (half + 1) * BANK_HEADS)
                flipped = psum.tile([P, BANK_HEADS, P], F32, tag="flip", bufs=3)
                for k in range(BANK_HEADS):
                    nc.tensor.transpose(
                        flipped[:, k, :],
                        block_of(b, i, j)[:, half * BANK_HEADS + k, :],
                        ident_f32[:],
                    )
                nc.scalar.copy(out=block_of(b, j, i)[:, heads, :], in_=flipped[:])

        def block_written(b, t, j):
            J = j // PANEL_TILES
            width = PANEL_TILES * P
            row_fill[b][J][t] += 1
            if row_fill[b][J][t] == PANEL_TILES:
                attn_rows = out_1[b].rearrange("n (t p) d -> p t n d", p=P)
                nc.sync.dma_start(
                    out=attn_rows[:, t, :, J * width : (J + 1) * width], in_=panel[b][J][:, t, :, :]
                )

        def mirror_and_store(u):
            b, i, j = UNITS[u]
            if i != j:
                mirror(u)
                block_written(b, j, i)
            block_written(b, i, j)

        def regroup(b, j, n0, engine):
            first = (j % PANEL_TILES) * P
            by_word = panel[b][j // PANEL_TILES][:, :, n0 : n0 + PIECE_HEADS, first : first + P]
            a_grouped = a_mx.tile([P, PIECE_HEADS, P, CT], BF16, align_bytes=64)
            copy_words(engine, a_grouped[:], by_word.rearrange("p t n c -> p n c t"))
            pieces[b, j, n0] = a_grouped

        def quantise(b, j, n0):
            a_codes = a_mx.tile([P, PIECE_HEADS * P], U32, align_bytes=64)
            a_scales = a_mx.tile([P, PIECE_HEADS * P], U8, align_bytes=64)
            nc.vector.quantize_mx(
                out=a_codes[:].bitcast(FP8X4),
                scales=a_scales[:],
                in_=pieces[b, j, n0][:].rearrange("p n c t -> p (n c t)"),
            )
            pieces[b, j, n0] = a_codes, a_scales

        def multiply_and_store(b, j, n0, engines, tag, tag_bufs):
            a_codes, a_scales = pieces[b, j, n0]
            tiles = PIECE_HEADS * KT
            accs = []
            for half in range(tiles // 4):
                acc = psum.tile([P, 4, P], F32, name="acc", tag=tag, bufs=tag_bufs)
                for k in range(4):
                    n = (half * 4 + k) // KT
                    m = n0 * KT + half * 4 + k
                    nc.tensor.matmul_mx(
                        out=acc[:, k, :],
                        lhsT=q_codes[b][:, m * P : (m + 1) * P].bitcast(FP8X4),
                        lhsT_scale=q_scales[b][:, m * P : (m + 1) * P],
                        rhs=a_codes[:, n * P : (n + 1) * P].bitcast(FP8X4),
                        rhs_scale=a_scales[:, n * P : (n + 1) * P],
                        start=True,
                        stop=True,
                    )
                accs.append(acc)
            J, first = j // PANEL_TILES, (j % PANEL_TILES) * P
            if (b, J) not in h_sb:
                h_sb[b, J] = large.tile(
                    [P, TOKEN_TILES, PANEL_TILES * P], F32, name="h_sb", tag="large"
                )
            for half in range(tiles // 4):
                m = n0 * KT + half * 4
                target = h_sb[b, J][:, m : m + 4, first : first + P]
                if engines[half] == "scalar":
                    nc.scalar.copy(out=target, in_=accs[half][:])
                else:
                    nc.vector.tensor_copy(out=target, in_=accs[half][:])
            h_fill[b, J, n0] = h_fill.get((b, J, n0), 0) + 1
            if h_fill[b, J, n0] == PANEL_TILES:
                h_rows = out_0[b].rearrange("(m w) c -> w m c", w=P)
                rows = slice(n0 * KT, n0 * KT + tiles)
                width = PANEL_TILES * P
                nc.sync.dma_start(
                    out=h_rows[:, rows, J * width : (J + 1) * width], in_=h_sb[b, J][:, rows, :]
                )

        for b in range(BATCH):
            load_q(b)

        writings = []

        def write_at(time, action, *args):
            writings.append((time, len(writings), action, args))

        write_at(0.25, invert_sharp)
        for u in range(len(UNITS)):
            write_at(u + SCORES, scores, u)
            write_at(u, subtract_maximum, u)
            write_at(u + EXPONENTIAL, exponential, u)
            write_at(u + ADD_HALVES, add_halves, u)
            write_at(u + SUM_HEADS, sum_heads, u)
            write_at(u + RECIPROCAL, reciprocal, u)
            write_at(u + NORMALISE, normalise, u)
            write_at(u + MIRROR, mirror_and_store, u)
        for b in range(BATCH):
            for t in range(CT):
                write_at(TURN_FIRST[b] + t, turn_q, b, t)
            for piece in range(Q_PIECES):
                time = Q_REGROUP_FIRST[b] + piece * Q_REGROUP_STEP[b]
                write_at(time, regroup_q, b, piece)
                write_at(time + Q_QUANTISE[b], quantise_q, b, piece)
            for j in range(CT):
                last = max(u for u in range(len(UNITS)) if UNITS[u][0] == b and j in UNITS[u][1:])
                ending = last >= len(UNITS) - 2
                for k in range(HEADS // PIECE_HEADS):
                    piece = (b, j, k * PIECE_HEADS)
                    time = last + (REGROUP_LAST if j == CT - 1 else REGROUP) + k * NEXT_PIECE
                    engine = LAST_REGROUP[j, k] if ending else "scalar"
                    write_at(time, regroup, *piece, engine)
                    write_at(time + QUANTISE, quantise, *piece)
                    engines = ("vector", "scalar") if b else ("scalar", "vector")
                    tag, tag_bufs = ("scores", 4) if ending else ("flip", 3)
                    write_at(time + MULTIPLY, multiply_and_store, *piece, engines, tag, tag_bufs)
        for time, index, action, args in sorted(writings, key=lambda writing: writing[:2]):
            action(*args)
